import numpy as np
import ml_dtypes


def mxq(x, axis, fmt="e4m3"):
    dtype, down = {"e4m3": (ml_dtypes.float8_e4m3fn, 7), "e5m2": (ml_dtypes.float8_e5m2, 14)}[fmt]
    v = np.moveaxis(np.asarray(x, np.float32).astype(ml_dtypes.bfloat16).astype(np.float64), axis, -1)
    blocks = v.reshape(v.shape[:-1] + (-1, 32))
    amax = np.abs(blocks).max(-1, keepdims=True)
    byte = np.maximum(np.where(amax > 0, np.frexp(amax)[1] - 1 + 127, 0) - down, 1)
    scale = np.exp2(byte - 127.0)
    codes = (blocks / scale).astype(np.float32).astype(dtype).astype(np.float64)
    return np.moveaxis((codes * scale).reshape(v.shape), -1, axis)


WIDE = False


def mx_kscale(k):
    if not WIDE:
        return np.ones(k)
    levels = np.array([10, -10, 5, -5, 0])
    if k % 512:
        return np.exp2(np.random.permutation(np.resize(levels, k // 32))).repeat(32)
    a = np.empty((k // 512, 16))
    for p in range(k // 512):
        a[p, :8] = np.random.permutation(np.resize(levels, 8))
        for g in range(8):
            far = levels[np.abs(levels - a[p, g]) >= 10]
            a[p, g + 8] = far[np.random.randint(len(far))]
    return np.exp2(a.ravel()).repeat(32)


BF16 = ml_dtypes.bfloat16


def bf(x):
    return np.asarray(x, np.float32).astype(BF16)


def f64(x):
    return np.asarray(x).astype(np.float64)


B, N, E, H, NOPE, VDIM, ROPE, QR, KVR = 4, 1024, 1024, 4, 64, 128, 32, 512, 512
QH = NOPE + ROPE
BASE = 10000.0


def rope(v):
    d = v.shape[-1]
    n = v.shape[-2]
    theta = BASE ** (-2.0 * np.arange(d // 2) / d)
    ang = np.arange(n)[:, None] * theta[None, :]
    cos, sin = np.cos(ang), np.sin(ang)
    v1, v2 = v[..., 0::2], v[..., 1::2]
    return np.stack([v1 * cos - v2 * sin, v1 * sin + v2 * cos], axis=-1).reshape(v.shape)


def setup_inputs():
    s, t = mx_kscale(E), mx_kscale(QR)
    return {"x": bf(np.random.standard_normal((B, N, E)) * s),
            "Wqa": bf(np.random.standard_normal((E, QR)) / np.sqrt(E) / s[:, None] * t),
            "Wqb": bf(np.random.standard_normal((QR, H * QH)) / np.sqrt(QR) / t[:, None])}


def reference(x, Wqa, Wqb):
    cq = mxq(f64(x), 2, "e4m3") @ mxq(f64(Wqa), 0, "e4m3")
    q = mxq(cq, 2, "e4m3") @ mxq(f64(Wqb), 0, "e4m3")
    q = q.reshape(B, N, H, QH).transpose(0, 2, 1, 3)
    return np.concatenate([q[..., :NOPE], rope(q[..., NOPE:])], axis=-1)

@@ -1,0 +1,319 @@
+import math
+from contextlib import ExitStack
+
+import concourse.mybir as mybir
+from concourse.masks import make_identity
+
+F32 = mybir.dt.float32
+BF16 = mybir.dt.bfloat16
+I32 = mybir.dt.int32
+U32 = mybir.dt.uint32
+U8 = mybir.dt.uint8
+FP8X4 = mybir.dt.float8_e4m3fn_x4
+ALU = mybir.AluOpType
+ACT = mybir.ActivationFunctionType
+
+P = 128
+PACK = 4
+BATCH, SEQ, EMB = 4, 1024, 1024
+HEADS, NOPE, ROPE = 4, 64, 32
+HEAD = NOPE + ROPE
+RANK = 512
+PAIRS = ROPE // 2
+BASE = 10000.0
+
+TILES = 4
+ROUND = TILES * P
+ROUNDS = BATCH * SEQ // ROUND
+ROUNDS_PER_SEQ = SEQ // ROUND
+PASSES_1 = EMB // (P * PACK)
+RANK_TILES = RANK // P
+BANKS = 8
+VECTOR_TILE = 1
+WORDS = EMB // 2
+PLAIN_COLS = HEADS * NOPE
+TURNED_COLS = HEADS * 2 * ROPE
+
+FLOPS = 2 * BATCH * SEQ * (EMB * RANK + RANK * HEADS * HEAD)
+
+TWO_PI = 2.0 * math.pi
+TWO_PI_HIGH = math.floor(TWO_PI * 8192.0) / 8192.0
+TWO_PI_LOW = TWO_PI - TWO_PI_HIGH
+PHASES = (0.5 * math.pi, math.pi, 0.0)
+
+
+def tile_multilatentattention_pa_t_kernel(tc, x, Wqa, Wqb, out):
+    nc = tc.nc
+    with ExitStack() as ctx:
+        keep = ctx.enter_context(tc.tile_pool(name="keep", bufs=1))
+        work = ctx.enter_context(tc.tile_pool(name="work", bufs=2))
+        psum = ctx.enter_context(tc.psum_pool(name="psum", bufs=1))
+        ctx.enter_context(tc.manual_schedule())
+
+        x_rounds = x.flatten_outer_dims().rearrange("(r p j) e -> r p (j e)", p=P, j=TILES)
+        x_sb = keep.tile([P, ROUNDS, TILES, EMB], BF16)
+        x_words = x_sb[:].bitcast(F32)
+        wa_raw = keep.tile([P, PASSES_1, PACK, RANK], BF16)
+        wb_raw = keep.tile([P, PACK, HEADS * HEAD], BF16)
+
+        def load_x(r):
+            nc.sync.dma_start(out=x_sb[:, r].rearrange("p j e -> p (j e)"), in_=x_rounds[r])
+
+        nc.sync.dma_start(
+            out=wa_raw[:].rearrange("p g t c -> p g (t c)"),
+            in_=Wqa.rearrange("(g p t) c -> p g (t c)", p=P, t=PACK),
+        )
+        load_x(0)
+        load_x(1)
+        nc.sync.dma_start(out=wb_raw[:], in_=Wqb.rearrange("(p t) n -> p t n", t=PACK))
+        for r in range(2, ROUNDS):
+            load_x(r)
+
+        zero = keep.tile([P, 1], F32)
+        nc.gpsimd.memset(zero[:], 0.0)
+        warm = keep.tile([P, 1], F32)
+        nc.scalar.activation(out=warm[:], in_=zero[:], func=ACT.Sin)
+
+        classes = ROUNDS_PER_SEQ * TILES
+        position = keep.tile([P, classes], F32)
+        nc.gpsimd.iota(
+            position[:],
+            pattern=[[ROUND, ROUNDS_PER_SEQ], [1, TILES]],
+            base=0,
+            channel_multiplier=TILES,
+            allow_small_or_imprecise_dtypes=True,
+        )
+        ident = keep.tile([P, P], F32)
+        make_identity(nc, ident[:])
+
+        plain_angle = keep.tile([P, PAIRS, classes], F32)
+        for i in range(PAIRS):
+            nc.vector.tensor_scalar(
+                out=plain_angle[:, i, :],
+                in0=position[:],
+                scalar1=BASE ** (-float(i) / PAIRS),
+                scalar2=None,
+                op0=ALU.mult,
+            )
+        angle = keep.tile([P, len(PHASES), PAIRS, classes], F32)
+        for s in range(len(PHASES)):
+            nc.vector.tensor_scalar(
+                out=angle[:, s], in0=plain_angle[:], scalar1=PHASES[s], scalar2=None, op0=ALU.add
+            )
+        turns_int = keep.tile([P, len(PHASES), PAIRS, classes], I32)
+        nc.vector.tensor_scalar(
+            out=turns_int[:], in0=angle[:], scalar1=1.0 / TWO_PI, scalar2=None, op0=ALU.mult
+        )
+        turns = keep.tile([P, len(PHASES), PAIRS, classes], F32)
+        nc.vector.tensor_copy(out=turns[:], in_=turns_int[:])
+        for part in (TWO_PI_HIGH, TWO_PI_LOW):
+            nc.vector.scalar_tensor_tensor(
+                out=angle[:], in0=turns[:], scalar=-part, in1=angle[:], op0=ALU.mult, op1=ALU.add
+            )
+        wrap = keep.tile([P, len(PHASES), PAIRS, classes], F32)
+        nc.vector.tensor_scalar(
+            out=wrap[:], in0=angle[:], scalar1=math.pi, scalar2=-TWO_PI, op0=ALU.is_gt, op1=ALU.mult
+        )
+        nc.vector.tensor_tensor(out=angle[:], in0=angle[:], in1=wrap[:], op=ALU.add)
+        nc.vector.tensor_scalar(
+            out=wrap[:], in0=angle[:], scalar1=-math.pi, scalar2=TWO_PI, op0=ALU.is_lt, op1=ALU.mult
+        )
+        nc.vector.tensor_tensor(out=angle[:], in0=angle[:], in1=wrap[:], op=ALU.add)
+        factors = keep.tile([P, classes, 2, PAIRS, 2], F32)
+        nc.scalar.activation(
+            out=factors[:, :, 0],
+            in_=angle[:, 0].rearrange("p i c -> p c i").unsqueeze(3).to_broadcast([P, classes, PAIRS, 2]),
+            func=ACT.Sin,
+        )
+        nc.scalar.activation(
+            out=factors[:, :, 1], in_=angle[:, 1:3].rearrange("p s i c -> p c i s"), func=ACT.Sin
+        )
+
+        wa_grouped = keep.tile([P, PASSES_1, RANK, PACK], BF16, align_bytes=64)
+        for g in range(PASSES_1):
+            nc.vector.tensor_copy(
+                out=wa_grouped[:, g].rearrange("p (t m) j -> p t m j", t=RANK_TILES),
+                in_=wa_raw[:, g].rearrange("p j (m t) -> p t m j", t=RANK_TILES),
+            )
+        wa_codes = keep.tile([P, PASSES_1, RANK], U32, align_bytes=64)
+        wa_scales = keep.tile([P, PASSES_1, RANK], U8, align_bytes=64)
+        nc.vector.quantize_mx(
+            out=wa_codes[:].rearrange("p g c -> p (g c)").bitcast(FP8X4),
+            scales=wa_scales[:].rearrange("p g c -> p (g c)"),
+            in_=wa_grouped[:].rearrange("p g c t -> p (g c t)"),
+        )
+
+        wb_codes = keep.tile([P, PLAIN_COLS + TURNED_COLS], U32, align_bytes=64)
+        wb_scales = keep.tile([P, PLAIN_COLS + TURNED_COLS], U8, align_bytes=64)
+
+        def prepare_wb():
+            wb_grouped = keep.tile([P, PLAIN_COLS + TURNED_COLS, PACK], BF16, align_bytes=64)
+            by_head = wb_raw[:].rearrange("p t (h f) -> p h f t", f=HEAD)
+            nc.vector.tensor_copy(
+                out=wb_grouped[:, 0:PLAIN_COLS, :].rearrange("p (h f) t -> p h f t", f=NOPE),
+                in_=by_head[:, :, 0:NOPE, :],
+            )
+            turned = wb_grouped[:, PLAIN_COLS:, :].rearrange("p (h s f) t -> p h s f t", s=2, f=ROPE)
+            nc.vector.tensor_copy(out=turned[:, :, 0], in_=by_head[:, :, NOPE:HEAD, :])
+            swapped = turned[:, :, 1].rearrange("p h (i e) t -> p h i e t", e=2)
+            pairs = by_head[:, :, NOPE:HEAD, :].rearrange("p h (i e) t -> p h i e t", e=2)
+            for e in range(2):
+                nc.vector.tensor_copy(out=swapped[:, :, :, e, :], in_=pairs[:, :, :, 1 - e, :])
+            nc.vector.quantize_mx(
+                out=wb_codes[:].bitcast(FP8X4),
+                scales=wb_scales[:],
+                in_=wb_grouped[:].rearrange("p c t -> p (c t)"),
+            )
+
+        banks_taken = []
+
+        def next_bank(shape):
+            tag = "bank%d" % (len(banks_taken) % BANKS)
+            bank = psum.tile(shape, F32, name=tag, tag=tag)
+            banks_taken.append(tag)
+            return bank
+
+        x_quantised = {}
+        cq_grouped = {}
+        cq_quantised = {}
+        results = {}
+
+        def transpose_x(r):
+            banks = []
+            for j in range(TILES):
+                xt = next_bank([P, PASSES_1 * 2, P])
+                for g in range(PASSES_1):
+                    for u in range(2):
+                        nc.tensor.transpose(
+                            xt[:, 2 * g + u, :],
+                            x_words[:, r, j, 2 * g * P + u : 2 * (g + 1) * P : 2],
+                            ident[:],
+                        )
+                banks.append(xt)
+            x_grouped = work.tile([P, TILES, PASSES_1, P, PACK], BF16, align_bytes=64)
+            x_codes = work.tile([P, TILES, PASSES_1, P], U32, align_bytes=64)
+            x_scales = work.tile([P, TILES, PASSES_1, P], U8, align_bytes=64)
+            x_quantised[r] = (x_codes, x_scales, x_grouped)
+            for half in range(2):
+                for j in range(2 * half, 2 * half + 2):
+                    nc.scalar.copy(
+                        out=x_grouped[:, j].bitcast(F32),
+                        in_=banks[j][:].rearrange("p (g u) n -> p g n u", u=2),
+                    )
+                if half == 0:
+                    quantise_x(r, half)
+
+        def quantise_x(r, half):
+            x_codes, x_scales, x_grouped = x_quantised[r]
+            two = slice(2 * half, 2 * half + 2)
+            nc.vector.quantize_mx(
+                out=x_codes[:, two].rearrange("p j g n -> p (j g n)").bitcast(FP8X4),
+                scales=x_scales[:, two].rearrange("p j g n -> p (j g n)"),
+                in_=x_grouped[:, two].rearrange("p j g n t -> p (j g n t)"),
+            )
+
+        def first_product(r, half):
+            x_codes, x_scales, x_grouped = x_quantised[r]
+            if half == 0:
+                cq_bf = work.tile([P, TILES, P, PACK], BF16, align_bytes=64)
+                cq_grouped[r] = cq_bf
+            for j in range(2 * half, 2 * half + 2):
+                cq_ps = next_bank([P, RANK_TILES, P])
+                for t in range(RANK_TILES):
+                    for g in range(PASSES_1):
+                        nc.tensor.matmul_mx(
+                            out=cq_ps[:, t, :],
+                            lhsT=wa_codes[:, g, t * P : (t + 1) * P].bitcast(FP8X4),
+                            lhsT_scale=wa_scales[:, g, t * P : (t + 1) * P],
+                            rhs=x_codes[:, j, g, :].bitcast(FP8X4),
+                            rhs_scale=x_scales[:, j, g, :],
+                            start=(g == 0),
+                            stop=(g == PASSES_1 - 1),
+                        )
+                if j == VECTOR_TILE:
+                    nc.vector.tensor_copy(out=cq_grouped[r][:, j], in_=cq_ps[:].rearrange("p t n -> p n t"))
+                else:
+                    nc.scalar.copy(out=cq_grouped[r][:, j], in_=cq_ps[:].rearrange("p t n -> p n t"))
+
+        def quantise_cq(r, half):
+            if half == 0:
+                cq_codes = work.tile([P, TILES, P], U32, align_bytes=64)
+                cq_scales = work.tile([P, TILES, P], U8, align_bytes=64)
+                cq_quantised[r] = (cq_codes, cq_scales)
+            cq_codes, cq_scales = cq_quantised[r]
+            two = slice(2 * half, 2 * half + 2)
+            nc.vector.quantize_mx(
+                out=cq_codes[:, two].rearrange("p j n -> p (j n)").bitcast(FP8X4),
+                scales=cq_scales[:, two].rearrange("p j n -> p (j n)"),
+                in_=cq_grouped[r][:, two].rearrange("p j n t -> p (j n t)"),
+            )
+
+        def second_product(r, half):
+            cq_codes, cq_scales = cq_quantised[r]
+            if half == 0:
+                products = work.tile([P, TILES, HEADS, 2, ROPE], F32)
+                o_sb = work.tile([P, HEADS, TILES, HEAD], F32, bufs=3)
+                results[r] = (products, o_sb)
+            products, o_sb = results[r]
+            two = slice(2 * half, 2 * half + 2)
+            plain_ps = next_bank([P, 2, PLAIN_COLS])
+            turned_ps = next_bank([P, 2, TURNED_COLS])
+            for jj in range(2):
+                j = 2 * half + jj
+                for bank, cols in ((plain_ps, slice(0, PLAIN_COLS)), (turned_ps, slice(PLAIN_COLS, PLAIN_COLS + TURNED_COLS))):
+                    nc.tensor.matmul_mx(
+                        out=bank[:, jj, :],
+                        lhsT=cq_codes[:, j, :].bitcast(FP8X4),
+                        lhsT_scale=cq_scales[:, j, :],
+                        rhs=wb_codes[:, cols].bitcast(FP8X4),
+                        rhs_scale=wb_scales[:, cols],
+                        start=True,
+                        stop=True,
+                    )
+            nc.scalar.copy(
+                out=o_sb[:, :, two, 0:NOPE].rearrange("p h j f -> p j h f"),
+                in_=plain_ps[:].rearrange("p j (h f) -> p j h f", f=NOPE),
+            )
+            first_class = (r % ROUNDS_PER_SEQ) * TILES + 2 * half
+            nc.vector.tensor_tensor(
+                out=products[:, two].rearrange("p j h s f -> p j h (s f)"),
+                in0=turned_ps[:].rearrange("p j (h f) -> p j h f", f=2 * ROPE),
+                in1=factors[:, first_class : first_class + 2]
+                .rearrange("p c s i e -> p c (s i e)")
+                .unsqueeze(2)
+                .to_broadcast([P, 2, HEADS, 2 * ROPE]),
+                op=ALU.mult,
+            )
+
+        def finish(r, half):
+            products, o_sb = results[r]
+            two = slice(2 * half, 2 * half + 2)
+            nc.vector.tensor_tensor(
+                out=o_sb[:, :, two, NOPE:HEAD].rearrange("p h j f -> p j h f"),
+                in0=products[:, two, :, 0, :],
+                in1=products[:, two, :, 1, :],
+                op=ALU.add,
+            )
+            b = r // ROUNDS_PER_SEQ
+            n0 = (r % ROUNDS_PER_SEQ) * ROUND
+            nc.sync.dma_start(
+                out=out[b, :, n0 : n0 + ROUND, :].rearrange("h (p j) f -> p h j f", j=TILES)[:, :, two, :],
+                in_=o_sb[:, :, two, :],
+            )
+
+        for s in range(ROUNDS + 2):
+            if s < ROUNDS:
+                transpose_x(s)
+            for half in range(2):
+                if 0 <= s - 1 < ROUNDS:
+                    first_product(s - 1, half)
+                if 0 <= s - 2:
+                    second_product(s - 2, half)
+                if 0 <= s - 1 < ROUNDS:
+                    quantise_cq(s - 1, half)
+                if 0 <= s - 2:
+                    finish(s - 2, half)
+                if half == 0 and s < ROUNDS:
+                    quantise_x(s, 1)
+            if s == 0:
+                prepare_wb()

@@ -24,50 +24,56 @@ BASE = 10000.0
 
 TILES = 4
 ROUND = TILES * P
-ROUNDS = BATCH * SEQ // ROUND
 ROUNDS_PER_SEQ = SEQ // ROUND
+PAIR = 2
+STEPS = BATCH * SEQ // (PAIR * P)
 PASSES_1 = EMB // (P * PACK)
 RANK_TILES = RANK // P
 BANKS = 8
-VECTOR_TILE = 1
 WORDS = EMB // 2
 PLAIN_COLS = HEADS * NOPE
-TURNED_COLS = HEADS * 2 * ROPE
+TURNED_COLS = HEADS * ROPE
 
 FLOPS = 2 * BATCH * SEQ * (EMB * RANK + RANK * HEADS * HEAD)
 
 TWO_PI = 2.0 * math.pi
 TWO_PI_HIGH = math.floor(TWO_PI * 8192.0) / 8192.0
 TWO_PI_LOW = TWO_PI - TWO_PI_HIGH
-PHASES = (0.5 * math.pi, math.pi, 0.0)
 
 
 def tile_multilatentattention_pa_t_kernel(tc, x, Wqa, Wqb, out):
     nc = tc.nc
     with ExitStack() as ctx:
         keep = ctx.enter_context(tc.tile_pool(name="keep", bufs=1))
-        work = ctx.enter_context(tc.tile_pool(name="work", bufs=2))
+        work = ctx.enter_context(tc.tile_pool(name="work", bufs=3))
         psum = ctx.enter_context(tc.psum_pool(name="psum", bufs=1))
         ctx.enter_context(tc.manual_schedule())
 
-        x_rounds = x.flatten_outer_dims().rearrange("(r p j) e -> r p (j e)", p=P, j=TILES)
-        x_sb = keep.tile([P, ROUNDS, TILES, EMB], BF16)
+        x_rounds = x.flatten_outer_dims().rearrange("(r p j) e -> r p j e", p=P, j=TILES)
+        x_sb = keep.tile([P, BATCH * SEQ // ROUND, TILES, EMB], BF16)
         x_words = x_sb[:].bitcast(F32)
         wa_raw = keep.tile([P, PASSES_1, PACK, RANK], BF16)
         wb_raw = keep.tile([P, PACK, HEADS * HEAD], BF16)
 
-        def load_x(r):
-            nc.sync.dma_start(out=x_sb[:, r].rearrange("p j e -> p (j e)"), in_=x_rounds[r])
+        def load_x(s, first, count):
+            r, j = s // 2, 2 * (s % 2) + first
+            nc.sync.dma_start(out=x_sb[:, r, j : j + count, :], in_=x_rounds[r][:, j : j + count, :])
 
-        nc.sync.dma_start(
-            out=wa_raw[:].rearrange("p g t c -> p g (t c)"),
-            in_=Wqa.rearrange("(g p t) c -> p g (t c)", p=P, t=PACK),
-        )
-        load_x(0)
-        load_x(1)
+        def load_wa(g):
+            nc.sync.dma_start(
+                out=wa_raw[:, g].rearrange("p t c -> p (t c)"),
+                in_=Wqa.rearrange("(g p t) c -> g p (t c)", p=P, t=PACK)[g],
+            )
+
+        load_x(0, 0, 1)
+        load_x(0, 1, 1)
+        load_wa(0)
+        load_wa(1)
+        load_x(1, 0, 2)
+        load_x(2, 0, 2)
         nc.sync.dma_start(out=wb_raw[:], in_=Wqb.rearrange("(p t) n -> p t n", t=PACK))
-        for r in range(2, ROUNDS):
-            load_x(r)
+        for s in range(3, STEPS):
+            load_x(s, 0, 2)
 
         zero = keep.tile([P, 1], F32)
         nc.gpsimd.memset(zero[:], 0.0)
@@ -86,62 +92,65 @@ def tile_multilatentattention_pa_t_kernel(tc, x, Wqa, Wqb, out):
         ident = keep.tile([P, P], F32)
         make_identity(nc, ident[:])
 
-        plain_angle = keep.tile([P, PAIRS, classes], F32)
+        angle = keep.tile([P, classes, PAIRS], F32)
         for i in range(PAIRS):
             nc.vector.tensor_scalar(
-                out=plain_angle[:, i, :],
+                out=angle[:, :, i],
                 in0=position[:],
                 scalar1=BASE ** (-float(i) / PAIRS),
                 scalar2=None,
                 op0=ALU.mult,
             )
-        angle = keep.tile([P, len(PHASES), PAIRS, classes], F32)
-        for s in range(len(PHASES)):
-            nc.vector.tensor_scalar(
-                out=angle[:, s], in0=plain_angle[:], scalar1=PHASES[s], scalar2=None, op0=ALU.add
-            )
-        turns_int = keep.tile([P, len(PHASES), PAIRS, classes], I32)
-        nc.vector.tensor_scalar(
-            out=turns_int[:], in0=angle[:], scalar1=1.0 / TWO_PI, scalar2=None, op0=ALU.mult
-        )
-        turns = keep.tile([P, len(PHASES), PAIRS, classes], F32)
+        turns_int = keep.tile([P, classes, PAIRS], I32)
+        nc.vector.tensor_scalar(out=turns_int[:], in0=angle[:], scalar1=1.0 / TWO_PI, scalar2=None, op0=ALU.mult)
+        turns = keep.tile([P, classes, PAIRS], F32)
         nc.vector.tensor_copy(out=turns[:], in_=turns_int[:])
-        for part in (TWO_PI_HIGH, TWO_PI_LOW):
-            nc.vector.scalar_tensor_tensor(
-                out=angle[:], in0=turns[:], scalar=-part, in1=angle[:], op0=ALU.mult, op1=ALU.add
-            )
-        wrap = keep.tile([P, len(PHASES), PAIRS, classes], F32)
-        nc.vector.tensor_scalar(
-            out=wrap[:], in0=angle[:], scalar1=math.pi, scalar2=-TWO_PI, op0=ALU.is_gt, op1=ALU.mult
-        )
-        nc.vector.tensor_tensor(out=angle[:], in0=angle[:], in1=wrap[:], op=ALU.add)
-        nc.vector.tensor_scalar(
-            out=wrap[:], in0=angle[:], scalar1=-math.pi, scalar2=TWO_PI, op0=ALU.is_lt, op1=ALU.mult
-        )
-        nc.vector.tensor_tensor(out=angle[:], in0=angle[:], in1=wrap[:], op=ALU.add)
+        wrap = keep.tile([P, classes, PAIRS], F32)
+
+        def add_multiple(values, factor, op0, scalar2):
+            if scalar2 is None:
+                nc.gpsimd.tensor_scalar(out=wrap[:], in0=values[:], scalar1=factor, scalar2=0.0, op0=ALU.mult, op1=ALU.add)
+            else:
+                nc.gpsimd.tensor_scalar(out=wrap[:], in0=values[:], scalar1=factor, scalar2=scalar2, op0=op0, op1=ALU.mult)
+            nc.gpsimd.tensor_tensor(out=angle[:], in0=angle[:], in1=wrap[:], op=ALU.add)
+
+        add_multiple(turns, -TWO_PI_HIGH, ALU.mult, None)
+        add_multiple(turns, -TWO_PI_LOW, ALU.mult, None)
+        add_multiple(angle, math.pi, ALU.is_gt, -TWO_PI)
+        add_multiple(angle, -math.pi, ALU.is_lt, TWO_PI)
+        size = keep.tile([P, classes, PAIRS], F32)
         factors = keep.tile([P, classes, 2, PAIRS, 2], F32)
-        nc.scalar.activation(
-            out=factors[:, :, 0],
-            in_=angle[:, 0].rearrange("p i c -> p c i").unsqueeze(3).to_broadcast([P, classes, PAIRS, 2]),
-            func=ACT.Sin,
-        )
-        nc.scalar.activation(
-            out=factors[:, :, 1], in_=angle[:, 1:3].rearrange("p s i c -> p c i s"), func=ACT.Sin
-        )
+
+        def make_factors():
+            nc.scalar.activation(out=size[:], in_=angle[:], func=ACT.Abs)
+            nc.scalar.activation(
+                out=factors[:, :, 0],
+                in_=size[:].unsqueeze(3).to_broadcast([P, classes, PAIRS, 2]),
+                func=ACT.Sin,
+                scale=-1.0,
+                bias=0.5 * math.pi,
+            )
+            for e, sign in ((0, 1.0), (1, -1.0)):
+                nc.scalar.activation(out=factors[:, :, 1, :, e], in_=angle[:], func=ACT.Sin, scale=sign)
 
         wa_grouped = keep.tile([P, PASSES_1, RANK, PACK], BF16, align_bytes=64)
-        for g in range(PASSES_1):
-            nc.vector.tensor_copy(
-                out=wa_grouped[:, g].rearrange("p (t m) j -> p t m j", t=RANK_TILES),
-                in_=wa_raw[:, g].rearrange("p j (m t) -> p t m j", t=RANK_TILES),
-            )
         wa_codes = keep.tile([P, PASSES_1, RANK], U32, align_bytes=64)
         wa_scales = keep.tile([P, PASSES_1, RANK], U8, align_bytes=64)
-        nc.vector.quantize_mx(
-            out=wa_codes[:].rearrange("p g c -> p (g c)").bitcast(FP8X4),
-            scales=wa_scales[:].rearrange("p g c -> p (g c)"),
-            in_=wa_grouped[:].rearrange("p g c t -> p (g c t)"),
-        )
+        HALF = RANK // 2
+
+        def regroup_wa(copy, g, half):
+            copy(
+                out=wa_grouped[:, g].rearrange("p (t m) j -> p t m j", t=RANK_TILES)[:, 2 * half : 2 * half + 2],
+                in_=wa_raw[:, g].rearrange("p j (m t) -> p t m j", t=RANK_TILES)[:, 2 * half : 2 * half + 2],
+            )
+
+        def quantise_wa(g, half):
+            cols = slice(half * HALF, (half + 1) * HALF)
+            nc.vector.quantize_mx(
+                out=wa_codes[:, g, cols].bitcast(FP8X4),
+                scales=wa_scales[:, g, cols],
+                in_=wa_grouped[:, g, cols].rearrange("p c t -> p (c t)"),
+            )
 
         wb_codes = keep.tile([P, PLAIN_COLS + TURNED_COLS], U32, align_bytes=64)
         wb_scales = keep.tile([P, PLAIN_COLS + TURNED_COLS], U8, align_bytes=64)
@@ -153,17 +162,16 @@ def tile_multilatentattention_pa_t_kernel(tc, x, Wqa, Wqb, out):
                 out=wb_grouped[:, 0:PLAIN_COLS, :].rearrange("p (h f) t -> p h f t", f=NOPE),
                 in_=by_head[:, :, 0:NOPE, :],
             )
-            turned = wb_grouped[:, PLAIN_COLS:, :].rearrange("p (h s f) t -> p h s f t", s=2, f=ROPE)
-            nc.vector.tensor_copy(out=turned[:, :, 0], in_=by_head[:, :, NOPE:HEAD, :])
-            swapped = turned[:, :, 1].rearrange("p h (i e) t -> p h i e t", e=2)
-            pairs = by_head[:, :, NOPE:HEAD, :].rearrange("p h (i e) t -> p h i e t", e=2)
-            for e in range(2):
-                nc.vector.tensor_copy(out=swapped[:, :, :, e, :], in_=pairs[:, :, :, 1 - e, :])
-            nc.vector.quantize_mx(
-                out=wb_codes[:].bitcast(FP8X4),
-                scales=wb_scales[:],
-                in_=wb_grouped[:].rearrange("p c t -> p (c t)"),
+            nc.vector.tensor_copy(
+                out=wb_grouped[:, PLAIN_COLS:, :].rearrange("p (h f) t -> p h f t", f=ROPE),
+                in_=by_head[:, :, NOPE:HEAD, :],
             )
+            for cols in (slice(0, PLAIN_COLS), slice(PLAIN_COLS, PLAIN_COLS + TURNED_COLS)):
+                nc.vector.quantize_mx(
+                    out=wb_codes[:, cols].bitcast(FP8X4),
+                    scales=wb_scales[:, cols],
+                    in_=wb_grouped[:, cols, :].rearrange("p c t -> p (c t)"),
+                )
 
         banks_taken = []
 
@@ -173,51 +181,42 @@ def tile_multilatentattention_pa_t_kernel(tc, x, Wqa, Wqb, out):
             banks_taken.append(tag)
             return bank
 
-        x_quantised = {}
-        cq_grouped = {}
-        cq_quantised = {}
-        results = {}
+        x_grouped, x_quantised = {}, {}
+        cq_grouped, cq_quantised = {}, {}
+        outputs, results = {}, {}
 
-        def transpose_x(r):
-            banks = []
-            for j in range(TILES):
+        def transpose_x(s):
+            grouped = work.tile([P, PAIR, PASSES_1, P, PACK], BF16, name="x_grouped", align_bytes=64)
+            x_grouped[s] = grouped
+            for jj in range(PAIR):
                 xt = next_bank([P, PASSES_1 * 2, P])
                 for g in range(PASSES_1):
                     for u in range(2):
                         nc.tensor.transpose(
                             xt[:, 2 * g + u, :],
-                            x_words[:, r, j, 2 * g * P + u : 2 * (g + 1) * P : 2],
+                            x_words[:, s // 2, 2 * (s % 2) + jj, 2 * g * P + u : 2 * (g + 1) * P : 2],
                             ident[:],
                         )
-                banks.append(xt)
-            x_grouped = work.tile([P, TILES, PASSES_1, P, PACK], BF16, align_bytes=64)
-            x_codes = work.tile([P, TILES, PASSES_1, P], U32, align_bytes=64)
-            x_scales = work.tile([P, TILES, PASSES_1, P], U8, align_bytes=64)
-            x_quantised[r] = (x_codes, x_scales, x_grouped)
-            for half in range(2):
-                for j in range(2 * half, 2 * half + 2):
-                    nc.scalar.copy(
-                        out=x_grouped[:, j].bitcast(F32),
-                        in_=banks[j][:].rearrange("p (g u) n -> p g n u", u=2),
-                    )
-                if half == 0:
-                    quantise_x(r, half)
+                nc.scalar.copy(
+                    out=grouped[:, jj].bitcast(F32),
+                    in_=xt[:].rearrange("p (g u) n -> p g n u", u=2),
+                )
 
-        def quantise_x(r, half):
-            x_codes, x_scales, x_grouped = x_quantised[r]
-            two = slice(2 * half, 2 * half + 2)
+        def quantise_x(s):
+            codes = work.tile([P, PAIR, PASSES_1, P], U32, name="x_codes", align_bytes=64)
+            scales = work.tile([P, PAIR, PASSES_1, P], U8, name="x_scales", align_bytes=64)
+            x_quantised[s] = (codes, scales)
             nc.vector.quantize_mx(
-                out=x_codes[:, two].rearrange("p j g n -> p (j g n)").bitcast(FP8X4),
-                scales=x_scales[:, two].rearrange("p j g n -> p (j g n)"),
-                in_=x_grouped[:, two].rearrange("p j g n t -> p (j g n t)"),
+                out=codes[:].rearrange("p j g n -> p (j g n)").bitcast(FP8X4),
+                scales=scales[:].rearrange("p j g n -> p (j g n)"),
+                in_=x_grouped[s][:].rearrange("p j g n t -> p (j g n t)"),
             )
 
-        def first_product(r, half):
-            x_codes, x_scales, x_grouped = x_quantised[r]
-            if half == 0:
-                cq_bf = work.tile([P, TILES, P, PACK], BF16, align_bytes=64)
-                cq_grouped[r] = cq_bf
-            for j in range(2 * half, 2 * half + 2):
+        def first_product(s):
+            codes, scales = x_quantised[s]
+            grouped = work.tile([P, PAIR, P, PACK], BF16, name="cq_grouped", align_bytes=64)
+            cq_grouped[s] = grouped
+            for jj in range(PAIR):
                 cq_ps = next_bank([P, RANK_TILES, P])
                 for t in range(RANK_TILES):
                     for g in range(PASSES_1):
@@ -225,95 +224,102 @@ def tile_multilatentattention_pa_t_kernel(tc, x, Wqa, Wqb, out):
                             out=cq_ps[:, t, :],
                             lhsT=wa_codes[:, g, t * P : (t + 1) * P].bitcast(FP8X4),
                             lhsT_scale=wa_scales[:, g, t * P : (t + 1) * P],
-                            rhs=x_codes[:, j, g, :].bitcast(FP8X4),
-                            rhs_scale=x_scales[:, j, g, :],
+                            rhs=codes[:, jj, g, :].bitcast(FP8X4),
+                            rhs_scale=scales[:, jj, g, :],
                             start=(g == 0),
                             stop=(g == PASSES_1 - 1),
                         )
-                if j == VECTOR_TILE:
-                    nc.vector.tensor_copy(out=cq_grouped[r][:, j], in_=cq_ps[:].rearrange("p t n -> p n t"))
-                else:
-                    nc.scalar.copy(out=cq_grouped[r][:, j], in_=cq_ps[:].rearrange("p t n -> p n t"))
+                copy = nc.scalar.copy if jj == 0 else nc.vector.tensor_copy
+                copy(out=grouped[:, jj], in_=cq_ps[:].rearrange("p t n -> p n t"))
 
-        def quantise_cq(r, half):
-            if half == 0:
-                cq_codes = work.tile([P, TILES, P], U32, align_bytes=64)
-                cq_scales = work.tile([P, TILES, P], U8, align_bytes=64)
-                cq_quantised[r] = (cq_codes, cq_scales)
-            cq_codes, cq_scales = cq_quantised[r]
-            two = slice(2 * half, 2 * half + 2)
+        def quantise_cq(s):
+            codes = work.tile([P, PAIR, P], U32, name="cq_codes", align_bytes=64)
+            scales = work.tile([P, PAIR, P], U8, name="cq_scales", align_bytes=64)
+            cq_quantised[s] = (codes, scales)
             nc.vector.quantize_mx(
-                out=cq_codes[:, two].rearrange("p j n -> p (j n)").bitcast(FP8X4),
-                scales=cq_scales[:, two].rearrange("p j n -> p (j n)"),
-                in_=cq_grouped[r][:, two].rearrange("p j n t -> p (j n t)"),
+                out=codes[:].rearrange("p j n -> p (j n)").bitcast(FP8X4),
+                scales=scales[:].rearrange("p j n -> p (j n)"),
+                in_=cq_grouped[s][:].rearrange("p j n t -> p (j n t)"),
             )
 
-        def second_product(r, half):
-            cq_codes, cq_scales = cq_quantised[r]
-            if half == 0:
-                products = work.tile([P, TILES, HEADS, 2, ROPE], F32)
-                o_sb = work.tile([P, HEADS, TILES, HEAD], F32, bufs=3)
-                results[r] = (products, o_sb)
-            products, o_sb = results[r]
-            two = slice(2 * half, 2 * half + 2)
-            plain_ps = next_bank([P, 2, PLAIN_COLS])
-            turned_ps = next_bank([P, 2, TURNED_COLS])
-            for jj in range(2):
-                j = 2 * half + jj
-                for bank, cols in ((plain_ps, slice(0, PLAIN_COLS)), (turned_ps, slice(PLAIN_COLS, PLAIN_COLS + TURNED_COLS))):
+        def second_product(s):
+            codes, scales = cq_quantised[s]
+            products = work.tile([P, PAIR, 2, TURNED_COLS], F32, name="products")
+            o_sb = work.tile([P, HEADS, PAIR, HEAD], F32, name="o_sb", bufs=8)
+            results[s] = (products, o_sb)
+            plain_ps = next_bank([P, PAIR, PLAIN_COLS])
+            turned_ps = next_bank([P, PAIR, TURNED_COLS])
+            for jj in range(PAIR):
+                for bank, cols in (
+                    (plain_ps, slice(0, PLAIN_COLS)),
+                    (turned_ps, slice(PLAIN_COLS, PLAIN_COLS + TURNED_COLS)),
+                ):
                     nc.tensor.matmul_mx(
                         out=bank[:, jj, :],
-                        lhsT=cq_codes[:, j, :].bitcast(FP8X4),
-                        lhsT_scale=cq_scales[:, j, :],
+                        lhsT=codes[:, jj, :].bitcast(FP8X4),
+                        lhsT_scale=scales[:, jj, :],
                         rhs=wb_codes[:, cols].bitcast(FP8X4),
                         rhs_scale=wb_scales[:, cols],
                         start=True,
                         stop=True,
                     )
             nc.scalar.copy(
-                out=o_sb[:, :, two, 0:NOPE].rearrange("p h j f -> p j h f"),
+                out=o_sb[:, :, :, 0:NOPE].rearrange("p h j f -> p j h f"),
                 in_=plain_ps[:].rearrange("p j (h f) -> p j h f", f=NOPE),
             )
-            first_class = (r % ROUNDS_PER_SEQ) * TILES + 2 * half
+            c = 2 * (s % (2 * ROUNDS_PER_SEQ))
             nc.vector.tensor_tensor(
-                out=products[:, two].rearrange("p j h s f -> p j h (s f)"),
-                in0=turned_ps[:].rearrange("p j (h f) -> p j h f", f=2 * ROPE),
-                in1=factors[:, first_class : first_class + 2]
-                .rearrange("p c s i e -> p c (s i e)")
+                out=products[:].rearrange("p j s (h f) -> p j s h f", f=ROPE),
+                in0=turned_ps[:]
+                .rearrange("p j (h f) -> p j h f", f=ROPE)
                 .unsqueeze(2)
-                .to_broadcast([P, 2, HEADS, 2 * ROPE]),
+                .to_broadcast([P, PAIR, 2, HEADS, ROPE]),
+                in1=factors[:, c : c + 2]
+                .rearrange("p c s i e -> p c s (i e)")
+                .unsqueeze(3)
+                .to_broadcast([P, PAIR, 2, HEADS, ROPE]),
                 op=ALU.mult,
             )
 
-        def finish(r, half):
-            products, o_sb = results[r]
-            two = slice(2 * half, 2 * half + 2)
-            nc.vector.tensor_tensor(
-                out=o_sb[:, :, two, NOPE:HEAD].rearrange("p h j f -> p j h f"),
-                in0=products[:, two, :, 0, :],
-                in1=products[:, two, :, 1, :],
+        def finish(s):
+            products, o_sb = results[s]
+            nc.gpsimd.tensor_tensor(
+                out=o_sb[:, :, :, NOPE:HEAD].rearrange("p h j (i e) -> p j h i e", e=2),
+                in0=products[:, :, 0].rearrange("p j (h i e) -> p j h i e", h=HEADS, e=2),
+                in1=products[:, :, 1].rearrange("p j (h i e) -> p j h i e", h=HEADS, e=2)[:, :, :, :, ::-1],
                 op=ALU.add,
             )
-            b = r // ROUNDS_PER_SEQ
-            n0 = (r % ROUNDS_PER_SEQ) * ROUND
+            b = s // (2 * ROUNDS_PER_SEQ)
+            n0 = (s // 2) % ROUNDS_PER_SEQ * ROUND
+            j = 2 * (s % 2)
             nc.sync.dma_start(
-                out=out[b, :, n0 : n0 + ROUND, :].rearrange("h (p j) f -> p h j f", j=TILES)[:, :, two, :],
-                in_=o_sb[:, :, two, :],
+                out=out[b, :, n0 : n0 + ROUND, :].rearrange("h (p j) f -> p h j f", j=TILES)[:, :, j : j + 2, :],
+                in_=o_sb[:],
             )
 
-        for s in range(ROUNDS + 2):
-            if s < ROUNDS:
+        for s in range(STEPS + 2):
+            if s < STEPS:
                 transpose_x(s)
-            for half in range(2):
-                if 0 <= s - 1 < ROUNDS:
-                    first_product(s - 1, half)
-                if 0 <= s - 2:
-                    second_product(s - 2, half)
-                if 0 <= s - 1 < ROUNDS:
-                    quantise_cq(s - 1, half)
-                if 0 <= s - 2:
-                    finish(s - 2, half)
-                if half == 0 and s < ROUNDS:
-                    quantise_x(s, 1)
             if s == 0:
+                regroup_wa(nc.scalar.copy, 0, 1)
+                regroup_wa(nc.scalar.copy, 1, 1)
+                regroup_wa(nc.vector.tensor_copy, 0, 0)
+                quantise_wa(0, 0)
+                quantise_x(0)
+                regroup_wa(nc.vector.tensor_copy, 1, 0)
+                quantise_wa(0, 1)
+                quantise_wa(1, 0)
+                quantise_wa(1, 1)
+            if s == 1:
+                make_factors()
+            if 0 <= s - 2:
+                quantise_cq(s - 2)
+            if 0 < s < STEPS:
+                quantise_x(s)
+            if s == 1:
                 prepare_wb()
+            if 0 <= s - 1 < STEPS:
+                first_product(s - 1)
+            if 0 <= s - 2:
+                second_product(s - 2)
+                finish(s - 2)

@@ -25,8 +25,8 @@ BASE = 10000.0
 TILES = 4
 ROUND = TILES * P
 ROUNDS_PER_SEQ = SEQ // ROUND
+ROUNDS = BATCH * SEQ // ROUND
 PAIR = 2
-STEPS = BATCH * SEQ // (PAIR * P)
 PASSES_1 = EMB // (P * PACK)
 RANK_TILES = RANK // P
 BANKS = 8
@@ -50,13 +50,12 @@ def tile_multilatentattention_pa_t_kernel(tc, x, Wqa, Wqb, out):
         ctx.enter_context(tc.manual_schedule())
 
         x_rounds = x.flatten_outer_dims().rearrange("(r p j) e -> r p j e", p=P, j=TILES)
-        x_sb = keep.tile([P, BATCH * SEQ // ROUND, TILES, EMB], BF16)
+        x_sb = keep.tile([P, ROUNDS, TILES, EMB], BF16)
         x_words = x_sb[:].bitcast(F32)
         wa_raw = keep.tile([P, PASSES_1, PACK, RANK], BF16)
         wb_raw = keep.tile([P, PACK, HEADS * HEAD], BF16)
 
-        def load_x(s, first, count):
-            r, j = s // 2, 2 * (s % 2) + first
+        def load_x(r, j, count):
             nc.sync.dma_start(out=x_sb[:, r, j : j + count, :], in_=x_rounds[r][:, j : j + count, :])
 
         def load_wa(g):
@@ -65,15 +64,17 @@ def tile_multilatentattention_pa_t_kernel(tc, x, Wqa, Wqb, out):
                 in_=Wqa.rearrange("(g p t) c -> g p (t c)", p=P, t=PACK)[g],
             )
 
-        load_x(0, 0, 1)
-        load_x(0, 1, 1)
         load_wa(0)
         load_wa(1)
+        load_x(0, 0, 1)
+        load_x(0, 1, 1)
+        load_x(0, 2, 2)
         load_x(1, 0, 2)
-        load_x(2, 0, 2)
+        load_x(1, 2, 2)
         nc.sync.dma_start(out=wb_raw[:], in_=Wqb.rearrange("(p t) n -> p t n", t=PACK))
-        for s in range(3, STEPS):
-            load_x(s, 0, 2)
+        for r in range(2, ROUNDS):
+            for j in (0, 2):
+                load_x(r, j, 2)
 
         zero = keep.tile([P, 1], F32)
         nc.gpsimd.memset(zero[:], 0.0)
@@ -181,42 +182,57 @@ def tile_multilatentattention_pa_t_kernel(tc, x, Wqa, Wqb, out):
             banks_taken.append(tag)
             return bank
 
+        x_sorted = {}
         x_grouped, x_quantised = {}, {}
         cq_grouped, cq_quantised = {}, {}
-        outputs, results = {}, {}
+        results = {}
 
-        def transpose_x(s):
-            grouped = work.tile([P, PAIR, PASSES_1, P, PACK], BF16, name="x_grouped", align_bytes=64)
-            x_grouped[s] = grouped
-            for jj in range(PAIR):
+        def sort_x(r, half):
+            if half == 0:
+                words = work.tile([P, 2, TILES, WORDS // 2], F32, name="x_sorted", bufs=2)
+                x_sorted[r] = words
+            two = slice(2 * half, 2 * half + 2)
+            nc.vector.tensor_copy(
+                out=x_sorted[r][:, :, two, :],
+                in_=x_words[:, r, two, :].rearrange("p j (w u) -> p u j w", u=2),
+            )
+
+        def transpose_x(r):
+            grouped = work.tile([P, TILES, PASSES_1, P, PACK], BF16, name="x_grouped", bufs=2, align_bytes=64)
+            x_grouped[r] = grouped
+            for j in range(TILES):
                 xt = next_bank([P, PASSES_1 * 2, P])
                 for g in range(PASSES_1):
                     for u in range(2):
-                        nc.tensor.transpose(
-                            xt[:, 2 * g + u, :],
-                            x_words[:, s // 2, 2 * (s % 2) + jj, 2 * g * P + u : 2 * (g + 1) * P : 2],
-                            ident[:],
-                        )
+                        if r in x_sorted:
+                            words = x_sorted[r][:, u, j, g * P : (g + 1) * P]
+                        else:
+                            words = x_words[:, r, j, 2 * g * P + u : 2 * (g + 1) * P : 2]
+                        nc.tensor.transpose(xt[:, 2 * g + u, :], words, ident[:])
                 nc.scalar.copy(
-                    out=grouped[:, jj].bitcast(F32),
+                    out=grouped[:, j].bitcast(F32),
                     in_=xt[:].rearrange("p (g u) n -> p g n u", u=2),
                 )
 
-        def quantise_x(s):
-            codes = work.tile([P, PAIR, PASSES_1, P], U32, name="x_codes", align_bytes=64)
-            scales = work.tile([P, PAIR, PASSES_1, P], U8, name="x_scales", align_bytes=64)
-            x_quantised[s] = (codes, scales)
+        def quantise_x(r, half):
+            if half == 0:
+                codes = work.tile([P, TILES, PASSES_1, P], U32, name="x_codes", bufs=2, align_bytes=64)
+                scales = work.tile([P, TILES, PASSES_1, P], U8, name="x_scales", bufs=2, align_bytes=64)
+                x_quantised[r] = (codes, scales)
+            codes, scales = x_quantised[r]
+            two = slice(2 * half, 2 * half + 2)
             nc.vector.quantize_mx(
-                out=codes[:].rearrange("p j g n -> p (j g n)").bitcast(FP8X4),
-                scales=scales[:].rearrange("p j g n -> p (j g n)"),
-                in_=x_grouped[s][:].rearrange("p j g n t -> p (j g n t)"),
+                out=codes[:, two].rearrange("p j g n -> p (j g n)").bitcast(FP8X4),
+                scales=scales[:, two].rearrange("p j g n -> p (j g n)"),
+                in_=x_grouped[r][:, two].rearrange("p j g n t -> p (j g n t)"),
             )
 
-        def first_product(s):
-            codes, scales = x_quantised[s]
-            grouped = work.tile([P, PAIR, P, PACK], BF16, name="cq_grouped", align_bytes=64)
-            cq_grouped[s] = grouped
-            for jj in range(PAIR):
+        def first_product(r, half):
+            codes, scales = x_quantised[r]
+            if half == 0:
+                grouped = work.tile([P, TILES, P, PACK], BF16, name="cq_grouped", bufs=2, align_bytes=64)
+                cq_grouped[r] = grouped
+            for j in range(2 * half, 2 * half + 2):
                 cq_ps = next_bank([P, RANK_TILES, P])
                 for t in range(RANK_TILES):
                     for g in range(PASSES_1):
@@ -224,40 +240,43 @@ def tile_multilatentattention_pa_t_kernel(tc, x, Wqa, Wqb, out):
                             out=cq_ps[:, t, :],
                             lhsT=wa_codes[:, g, t * P : (t + 1) * P].bitcast(FP8X4),
                             lhsT_scale=wa_scales[:, g, t * P : (t + 1) * P],
-                            rhs=codes[:, jj, g, :].bitcast(FP8X4),
-                            rhs_scale=scales[:, jj, g, :],
+                            rhs=codes[:, j, g, :].bitcast(FP8X4),
+                            rhs_scale=scales[:, j, g, :],
                             start=(g == 0),
                             stop=(g == PASSES_1 - 1),
                         )
-                copy = nc.scalar.copy if jj == 0 else nc.vector.tensor_copy
-                copy(out=grouped[:, jj], in_=cq_ps[:].rearrange("p t n -> p n t"))
+                copy = nc.vector.tensor_copy if j == 1 else nc.scalar.copy
+                copy(out=cq_grouped[r][:, j], in_=cq_ps[:].rearrange("p t n -> p n t"))
 
-        def quantise_cq(s):
-            codes = work.tile([P, PAIR, P], U32, name="cq_codes", align_bytes=64)
-            scales = work.tile([P, PAIR, P], U8, name="cq_scales", align_bytes=64)
-            cq_quantised[s] = (codes, scales)
+        def quantise_cq(r, half):
+            if half == 0:
+                codes = work.tile([P, TILES, P], U32, name="cq_codes", align_bytes=64)
+                scales = work.tile([P, TILES, P], U8, name="cq_scales", align_bytes=64)
+                cq_quantised[r] = (codes, scales)
+            codes, scales = cq_quantised[r]
+            two = slice(2 * half, 2 * half + 2)
             nc.vector.quantize_mx(
-                out=codes[:].rearrange("p j n -> p (j n)").bitcast(FP8X4),
-                scales=scales[:].rearrange("p j n -> p (j n)"),
-                in_=cq_grouped[s][:].rearrange("p j n t -> p (j n t)"),
+                out=codes[:, two].rearrange("p j n -> p (j n)").bitcast(FP8X4),
+                scales=scales[:, two].rearrange("p j n -> p (j n)"),
+                in_=cq_grouped[r][:, two].rearrange("p j n t -> p (j n t)"),
             )
 
-        def second_product(s):
-            codes, scales = cq_quantised[s]
-            products = work.tile([P, PAIR, 2, TURNED_COLS], F32, name="products")
+        def second_product(r, half):
+            codes, scales = cq_quantised[r]
             o_sb = work.tile([P, HEADS, PAIR, HEAD], F32, name="o_sb", bufs=8)
-            results[s] = (products, o_sb)
             plain_ps = next_bank([P, PAIR, PLAIN_COLS])
             turned_ps = next_bank([P, PAIR, TURNED_COLS])
+            results[r, half] = (turned_ps, o_sb)
             for jj in range(PAIR):
+                j = 2 * half + jj
                 for bank, cols in (
                     (plain_ps, slice(0, PLAIN_COLS)),
                     (turned_ps, slice(PLAIN_COLS, PLAIN_COLS + TURNED_COLS)),
                 ):
                     nc.tensor.matmul_mx(
                         out=bank[:, jj, :],
-                        lhsT=codes[:, jj, :].bitcast(FP8X4),
-                        lhsT_scale=scales[:, jj, :],
+                        lhsT=codes[:, j, :].bitcast(FP8X4),
+                        lhsT_scale=scales[:, j, :],
                         rhs=wb_codes[:, cols].bitcast(FP8X4),
                         rhs_scale=wb_scales[:, cols],
                         start=True,
@@ -267,7 +286,11 @@ def tile_multilatentattention_pa_t_kernel(tc, x, Wqa, Wqb, out):
                 out=o_sb[:, :, :, 0:NOPE].rearrange("p h j f -> p j h f"),
                 in_=plain_ps[:].rearrange("p j (h f) -> p j h f", f=NOPE),
             )
-            c = 2 * (s % (2 * ROUNDS_PER_SEQ))
+
+        def rotate(r, half):
+            turned_ps, o_sb = results[r, half]
+            products = work.tile([P, PAIR, 2, TURNED_COLS], F32, name="products")
+            c = (r % ROUNDS_PER_SEQ) * TILES + 2 * half
             nc.vector.tensor_tensor(
                 out=products[:].rearrange("p j s (h f) -> p j s h f", f=ROPE),
                 in0=turned_ps[:]
@@ -280,46 +303,62 @@ def tile_multilatentattention_pa_t_kernel(tc, x, Wqa, Wqb, out):
                 .to_broadcast([P, PAIR, 2, HEADS, ROPE]),
                 op=ALU.mult,
             )
-
-        def finish(s):
-            products, o_sb = results[s]
-            nc.gpsimd.tensor_tensor(
+            adder = nc.vector if (r, half) == (ROUNDS - 1, 1) else nc.gpsimd
+            adder.tensor_tensor(
                 out=o_sb[:, :, :, NOPE:HEAD].rearrange("p h j (i e) -> p j h i e", e=2),
                 in0=products[:, :, 0].rearrange("p j (h i e) -> p j h i e", h=HEADS, e=2),
                 in1=products[:, :, 1].rearrange("p j (h i e) -> p j h i e", h=HEADS, e=2)[:, :, :, :, ::-1],
                 op=ALU.add,
             )
-            b = s // (2 * ROUNDS_PER_SEQ)
-            n0 = (s // 2) % ROUNDS_PER_SEQ * ROUND
-            j = 2 * (s % 2)
+            b = r // ROUNDS_PER_SEQ
+            n0 = (r % ROUNDS_PER_SEQ) * ROUND
+            two = slice(2 * half, 2 * half + 2)
             nc.sync.dma_start(
-                out=out[b, :, n0 : n0 + ROUND, :].rearrange("h (p j) f -> p h j f", j=TILES)[:, :, j : j + 2, :],
+                out=out[b, :, n0 : n0 + ROUND, :].rearrange("h (p j) f -> p h j f", j=TILES)[:, :, two, :],
                 in_=o_sb[:],
             )
 
-        for s in range(STEPS + 2):
-            if s < STEPS:
-                transpose_x(s)
-            if s == 0:
-                regroup_wa(nc.scalar.copy, 0, 1)
-                regroup_wa(nc.scalar.copy, 1, 1)
-                regroup_wa(nc.vector.tensor_copy, 0, 0)
-                quantise_wa(0, 0)
-                quantise_x(0)
-                regroup_wa(nc.vector.tensor_copy, 1, 0)
-                quantise_wa(0, 1)
-                quantise_wa(1, 0)
-                quantise_wa(1, 1)
-            if s == 1:
+        regroup_wa(nc.vector.tensor_copy, 0, 0)
+        regroup_wa(nc.vector.tensor_copy, 0, 1)
+        quantise_wa(0, 0)
+        quantise_wa(0, 1)
+        regroup_wa(nc.scalar.copy, 1, 1)
+        regroup_wa(nc.vector.tensor_copy, 1, 0)
+        quantise_wa(1, 0)
+        quantise_wa(1, 1)
+        transpose_x(0)
+        for half in range(2):
+            quantise_x(0, half)
+            sort_x(1, half)
+
+        for r in range(ROUNDS + 1):
+            here, ahead, sort, behind = r < ROUNDS, r + 1 < ROUNDS, r + 2 < ROUNDS, 0 <= r - 1
+            if behind:
+                rotate(r - 1, 0)
+                quantise_cq(r - 1, 1)
+            if here:
+                first_product(r, 0)
+            if behind:
+                second_product(r - 1, 1)
+                rotate(r - 1, 1)
+            if r == 0:
                 make_factors()
-            if 0 <= s - 2:
-                quantise_cq(s - 2)
-            if 0 < s < STEPS:
-                quantise_x(s)
-            if s == 1:
+            elif sort:
+                sort_x(r + 2, 0)
+            if here:
+                quantise_cq(r, 0)
+            if r == 0:
                 prepare_wb()
-            if 0 <= s - 1 < STEPS:
-                first_product(s - 1)
-            if 0 <= s - 2:
-                second_product(s - 2)
-                finish(s - 2)
+            if ahead:
+                transpose_x(r + 1)
+                quantise_x(r + 1, 0)
+            if r > 0 and sort:
+                sort_x(r + 2, 1)
+            if ahead:
+                quantise_x(r + 1, 1)
+            if r == 0:
+                for half in range(2):
+                    sort_x(2, half)
+            if here:
+                first_product(r, 1)
+                second_product(r, 0)

@@ -51,7 +51,6 @@ def tile_multilatentattention_pa_t_kernel(tc, x, Wqa, Wqb, out):
 
         x_rounds = x.flatten_outer_dims().rearrange("(r p j) e -> r p j e", p=P, j=TILES)
         x_sb = keep.tile([P, ROUNDS, TILES, EMB], BF16)
-        x_words = x_sb[:].bitcast(F32)
         wa_raw = keep.tile([P, PASSES_1, PACK, RANK], BF16)
         wb_raw = keep.tile([P, PACK, HEADS * HEAD], BF16)
 
@@ -59,19 +58,22 @@ def tile_multilatentattention_pa_t_kernel(tc, x, Wqa, Wqb, out):
             nc.sync.dma_start(out=x_sb[:, r, j : j + count, :], in_=x_rounds[r][:, j : j + count, :])
 
         def load_wa(g):
-            nc.sync.dma_start(
-                out=wa_raw[:, g].rearrange("p t c -> p (t c)"),
-                in_=Wqa.rearrange("(g p t) c -> g p (t c)", p=P, t=PACK)[g],
-            )
+            rows = Wqa.rearrange("(g q u i e) c -> g i q u (e c)", g=PASSES_1, u=2, i=2, e=2)
+            for i in range(2):
+                nc.sync.dma_start(
+                    out=wa_raw[i::2, g].rearrange("p (u e) c -> p u (e c)", e=2),
+                    in_=rows[g, i],
+                )
 
+        load_x(0, 0, 2)
         load_wa(0)
         load_wa(1)
-        load_x(0, 0, 1)
-        load_x(0, 1, 1)
         load_x(0, 2, 2)
         load_x(1, 0, 2)
+        rows = Wqb.rearrange("(q t i) n -> i q t n", t=PACK, i=4)
+        for i in range(4):
+            nc.sync.dma_start(out=wb_raw[i::4], in_=rows[i])
         load_x(1, 2, 2)
-        nc.sync.dma_start(out=wb_raw[:], in_=Wqb.rearrange("(p t) n -> p t n", t=PACK))
         for r in range(2, ROUNDS):
             for j in (0, 2):
                 load_x(r, j, 2)
@@ -131,7 +133,7 @@ def tile_multilatentattention_pa_t_kernel(tc, x, Wqa, Wqb, out):
                 scale=-1.0,
                 bias=0.5 * math.pi,
             )
-            for e, sign in ((0, 1.0), (1, -1.0)):
+            for e, sign in ((0, -1.0), (1, 1.0)):
                 nc.scalar.activation(out=factors[:, :, 1, :, e], in_=angle[:], func=ACT.Sin, scale=sign)
 
         wa_grouped = keep.tile([P, PASSES_1, RANK, PACK], BF16, align_bytes=64)
@@ -139,10 +141,13 @@ def tile_multilatentattention_pa_t_kernel(tc, x, Wqa, Wqb, out):
         wa_scales = keep.tile([P, PASSES_1, RANK], U8, align_bytes=64)
         HALF = RANK // 2
 
+        def copy_on_gpsimd(out, in_):
+            nc.gpsimd.tensor_scalar(out=out, in0=in_, scalar1=1.0, scalar2=0.0, op0=ALU.mult, op1=ALU.add)
+
         def regroup_wa(copy, g, half):
             copy(
-                out=wa_grouped[:, g].rearrange("p (t m) j -> p t m j", t=RANK_TILES)[:, 2 * half : 2 * half + 2],
-                in_=wa_raw[:, g].rearrange("p j (m t) -> p t m j", t=RANK_TILES)[:, 2 * half : 2 * half + 2],
+                out=wa_grouped[:, g].rearrange("p (t q i) j -> p t q j i", t=RANK_TILES, i=4)[:, 2 * half : 2 * half + 2],
+                in_=wa_raw[:, g].rearrange("p j (q t i) -> p t q j i", t=RANK_TILES, i=4)[:, 2 * half : 2 * half + 2],
             )
 
         def quantise_wa(g, half):
@@ -156,17 +161,20 @@ def tile_multilatentattention_pa_t_kernel(tc, x, Wqa, Wqb, out):
         wb_codes = keep.tile([P, PLAIN_COLS + TURNED_COLS], U32, align_bytes=64)
         wb_scales = keep.tile([P, PLAIN_COLS + TURNED_COLS], U8, align_bytes=64)
 
-        def prepare_wb():
-            wb_grouped = keep.tile([P, PLAIN_COLS + TURNED_COLS, PACK], BF16, align_bytes=64)
+        wb_grouped = keep.tile([P, PLAIN_COLS + TURNED_COLS, PACK], BF16, align_bytes=64)
+
+        def regroup_wb():
             by_head = wb_raw[:].rearrange("p t (h f) -> p h f t", f=HEAD)
-            nc.vector.tensor_copy(
+            copy_on_gpsimd(
                 out=wb_grouped[:, 0:PLAIN_COLS, :].rearrange("p (h f) t -> p h f t", f=NOPE),
                 in_=by_head[:, :, 0:NOPE, :],
             )
-            nc.vector.tensor_copy(
+            copy_on_gpsimd(
                 out=wb_grouped[:, PLAIN_COLS:, :].rearrange("p (h f) t -> p h f t", f=ROPE),
                 in_=by_head[:, :, NOPE:HEAD, :],
             )
+
+        def quantise_wb():
             for cols in (slice(0, PLAIN_COLS), slice(PLAIN_COLS, PLAIN_COLS + TURNED_COLS)):
                 nc.vector.quantize_mx(
                     out=wb_codes[:, cols].bitcast(FP8X4),
@@ -188,29 +196,25 @@ def tile_multilatentattention_pa_t_kernel(tc, x, Wqa, Wqb, out):
         results = {}
 
         def sort_x(r, half):
-            if half == 0:
-                words = work.tile([P, 2, TILES, WORDS // 2], F32, name="x_sorted", bufs=2)
-                x_sorted[r] = words
-            two = slice(2 * half, 2 * half + 2)
+            sorted_x = work.tile([P, 2, PAIR, WORDS], BF16, name="x_sorted", bufs=4)
+            x_sorted[r, half] = sorted_x
             nc.vector.tensor_copy(
-                out=x_sorted[r][:, :, two, :],
-                in_=x_words[:, r, two, :].rearrange("p j (w u) -> p u j w", u=2),
+                out=sorted_x[:].rearrange("p u j (q i) -> p u j q i", i=4),
+                in_=x_sb[:, r, 2 * half : 2 * half + 2, :].rearrange("p j (q u i) -> p u j q i", u=2, i=4),
             )
 
-        def transpose_x(r):
-            grouped = work.tile([P, TILES, PASSES_1, P, PACK], BF16, name="x_grouped", bufs=2, align_bytes=64)
-            x_grouped[r] = grouped
-            for j in range(TILES):
+        def transpose_x(r, half):
+            if half == 0:
+                grouped = work.tile([P, TILES, PASSES_1, P, PACK], BF16, name="x_grouped", bufs=2, align_bytes=64)
+                x_grouped[r] = grouped
+            words = x_sorted[r, half][:].bitcast(F32)
+            for jj in range(PAIR):
                 xt = next_bank([P, PASSES_1 * 2, P])
                 for g in range(PASSES_1):
                     for u in range(2):
-                        if r in x_sorted:
-                            words = x_sorted[r][:, u, j, g * P : (g + 1) * P]
-                        else:
-                            words = x_words[:, r, j, 2 * g * P + u : 2 * (g + 1) * P : 2]
-                        nc.tensor.transpose(xt[:, 2 * g + u, :], words, ident[:])
+                        nc.tensor.transpose(xt[:, 2 * g + u, :], words[:, u, jj, g * P : (g + 1) * P], ident[:])
                 nc.scalar.copy(
-                    out=grouped[:, j].bitcast(F32),
+                    out=x_grouped[r][:, 2 * half + jj].bitcast(F32),
                     in_=xt[:].rearrange("p (g u) n -> p g n u", u=2),
                 )
 
@@ -291,23 +295,22 @@ def tile_multilatentattention_pa_t_kernel(tc, x, Wqa, Wqb, out):
             turned_ps, o_sb = results[r, half]
             products = work.tile([P, PAIR, 2, TURNED_COLS], F32, name="products")
             c = (r % ROUNDS_PER_SEQ) * TILES + 2 * half
+            results[r, half] = (products, o_sb)
+            rotated = turned_ps[:].rearrange("p j (h i e) -> p j h i e", h=HEADS, e=2)
+            for s, source in ((0, rotated), (1, rotated[:, :, :, :, ::-1])):
+                nc.vector.tensor_tensor(
+                    out=products[:, :, s].rearrange("p j (h i e) -> p j h i e", h=HEADS, e=2),
+                    in0=source,
+                    in1=factors[:, c : c + 2, s].unsqueeze(2).to_broadcast([P, PAIR, HEADS, PAIRS, 2]),
+                    op=ALU.mult,
+                )
+
+        def finish(r, half):
+            products, o_sb = results[r, half]
             nc.vector.tensor_tensor(
-                out=products[:].rearrange("p j s (h f) -> p j s h f", f=ROPE),
-                in0=turned_ps[:]
-                .rearrange("p j (h f) -> p j h f", f=ROPE)
-                .unsqueeze(2)
-                .to_broadcast([P, PAIR, 2, HEADS, ROPE]),
-                in1=factors[:, c : c + 2]
-                .rearrange("p c s i e -> p c s (i e)")
-                .unsqueeze(3)
-                .to_broadcast([P, PAIR, 2, HEADS, ROPE]),
-                op=ALU.mult,
-            )
-            adder = nc.vector if (r, half) == (ROUNDS - 1, 1) else nc.gpsimd
-            adder.tensor_tensor(
-                out=o_sb[:, :, :, NOPE:HEAD].rearrange("p h j (i e) -> p j h i e", e=2),
-                in0=products[:, :, 0].rearrange("p j (h i e) -> p j h i e", h=HEADS, e=2),
-                in1=products[:, :, 1].rearrange("p j (h i e) -> p j h i e", h=HEADS, e=2)[:, :, :, :, ::-1],
+                out=o_sb[:, :, :, NOPE:HEAD].rearrange("p h j f -> p j h f"),
+                in0=products[:, :, 0].rearrange("p j (h f) -> p j h f", h=HEADS),
+                in1=products[:, :, 1].rearrange("p j (h f) -> p j h f", h=HEADS),
                 op=ALU.add,
             )
             b = r // ROUNDS_PER_SEQ
@@ -318,6 +321,8 @@ def tile_multilatentattention_pa_t_kernel(tc, x, Wqa, Wqb, out):
                 in_=o_sb[:],
             )
 
+        sort_x(0, 0)
+        transpose_x(0, 0)
         regroup_wa(nc.vector.tensor_copy, 0, 0)
         regroup_wa(nc.vector.tensor_copy, 0, 1)
         quantise_wa(0, 0)
@@ -326,16 +331,17 @@ def tile_multilatentattention_pa_t_kernel(tc, x, Wqa, Wqb, out):
         regroup_wa(nc.vector.tensor_copy, 1, 0)
         quantise_wa(1, 0)
         quantise_wa(1, 1)
-        transpose_x(0)
-        for half in range(2):
-            quantise_x(0, half)
-            sort_x(1, half)
+        quantise_x(0, 0)
+        sort_x(0, 1)
+        sort_x(1, 0)
+        regroup_wb()
 
         for r in range(ROUNDS + 1):
             here, ahead, sort, behind = r < ROUNDS, r + 1 < ROUNDS, r + 2 < ROUNDS, 0 <= r - 1
             if behind:
                 rotate(r - 1, 0)
                 quantise_cq(r - 1, 1)
+                finish(r - 1, 0)
             if here:
                 first_product(r, 0)
             if behind:
@@ -343,16 +349,23 @@ def tile_multilatentattention_pa_t_kernel(tc, x, Wqa, Wqb, out):
                 rotate(r - 1, 1)
             if r == 0:
                 make_factors()
+                transpose_x(0, 1)
+                sort_x(1, 1)
             elif sort:
                 sort_x(r + 2, 0)
             if here:
                 quantise_cq(r, 0)
             if r == 0:
-                prepare_wb()
+                quantise_x(0, 1)
+            if behind:
+                finish(r - 1, 1)
             if ahead:
-                transpose_x(r + 1)
+                transpose_x(r + 1, 0)
+                transpose_x(r + 1, 1)
                 quantise_x(r + 1, 0)
-            if r > 0 and sort:
+            if r == 0:
+                quantise_wb()
+            elif sort:
                 sort_x(r + 2, 1)
             if ahead:
                 quantise_x(r + 1, 1)

@@ -70,13 +70,12 @@ def tile_multilatentattention_pa_t_kernel(tc, x, Wqa, Wqb, out):
         load_wa(1)
         load_x(0, 2, 2)
         load_x(1, 0, 2)
+        load_x(1, 2, 2)
         rows = Wqb.rearrange("(q t i) n -> i q t n", t=PACK, i=4)
         for i in range(4):
             nc.sync.dma_start(out=wb_raw[i::4], in_=rows[i])
-        load_x(1, 2, 2)
         for r in range(2, ROUNDS):
-            for j in (0, 2):
-                load_x(r, j, 2)
+            load_x(r, 0, TILES)
 
         zero = keep.tile([P, 1], F32)
         nc.gpsimd.memset(zero[:], 0.0)
@@ -195,48 +194,49 @@ def tile_multilatentattention_pa_t_kernel(tc, x, Wqa, Wqb, out):
         cq_grouped, cq_quantised = {}, {}
         results = {}
 
-        def sort_x(r, half):
-            sorted_x = work.tile([P, 2, PAIR, WORDS], BF16, name="x_sorted", bufs=4)
-            x_sorted[r, half] = sorted_x
+        def sort_x(r, j0, j1):
+            sorted_x = work.tile([P, 2, j1 - j0, WORDS], BF16, name="x_sorted", tag="x_sorted%d" % (j1 - j0), bufs=2)
+            for j in range(j0, j1):
+                x_sorted[r, j] = (sorted_x, j - j0)
             nc.vector.tensor_copy(
                 out=sorted_x[:].rearrange("p u j (q i) -> p u j q i", i=4),
-                in_=x_sb[:, r, 2 * half : 2 * half + 2, :].rearrange("p j (q u i) -> p u j q i", u=2, i=4),
+                in_=x_sb[:, r, j0:j1, :].rearrange("p j (q u i) -> p u j q i", u=2, i=4),
             )
 
-        def transpose_x(r, half):
-            if half == 0:
+        def transpose_x(r, j0, j1):
+            if j0 == 0:
                 grouped = work.tile([P, TILES, PASSES_1, P, PACK], BF16, name="x_grouped", bufs=2, align_bytes=64)
                 x_grouped[r] = grouped
-            words = x_sorted[r, half][:].bitcast(F32)
-            for jj in range(PAIR):
+            for j in range(j0, j1):
+                sorted_x, place = x_sorted[r, j]
+                words = sorted_x[:].bitcast(F32)
                 xt = next_bank([P, PASSES_1 * 2, P])
                 for g in range(PASSES_1):
                     for u in range(2):
-                        nc.tensor.transpose(xt[:, 2 * g + u, :], words[:, u, jj, g * P : (g + 1) * P], ident[:])
+                        nc.tensor.transpose(xt[:, 2 * g + u, :], words[:, u, place, g * P : (g + 1) * P], ident[:])
                 nc.scalar.copy(
-                    out=x_grouped[r][:, 2 * half + jj].bitcast(F32),
+                    out=x_grouped[r][:, j].bitcast(F32),
                     in_=xt[:].rearrange("p (g u) n -> p g n u", u=2),
                 )
 
-        def quantise_x(r, half):
-            if half == 0:
+        def quantise_x(r, j0, j1):
+            if j0 == 0:
                 codes = work.tile([P, TILES, PASSES_1, P], U32, name="x_codes", bufs=2, align_bytes=64)
                 scales = work.tile([P, TILES, PASSES_1, P], U8, name="x_scales", bufs=2, align_bytes=64)
                 x_quantised[r] = (codes, scales)
             codes, scales = x_quantised[r]
-            two = slice(2 * half, 2 * half + 2)
             nc.vector.quantize_mx(
-                out=codes[:, two].rearrange("p j g n -> p (j g n)").bitcast(FP8X4),
-                scales=scales[:, two].rearrange("p j g n -> p (j g n)"),
-                in_=x_grouped[r][:, two].rearrange("p j g n t -> p (j g n t)"),
+                out=codes[:, j0:j1].rearrange("p j g n -> p (j g n)").bitcast(FP8X4),
+                scales=scales[:, j0:j1].rearrange("p j g n -> p (j g n)"),
+                in_=x_grouped[r][:, j0:j1].rearrange("p j g n t -> p (j g n t)"),
             )
 
-        def first_product(r, half):
+        def first_product(r, j0, j1):
             codes, scales = x_quantised[r]
-            if half == 0:
+            if j0 == 0:
                 grouped = work.tile([P, TILES, P, PACK], BF16, name="cq_grouped", bufs=2, align_bytes=64)
                 cq_grouped[r] = grouped
-            for j in range(2 * half, 2 * half + 2):
+            for j in range(j0, j1):
                 cq_ps = next_bank([P, RANK_TILES, P])
                 for t in range(RANK_TILES):
                     for g in range(PASSES_1):
@@ -252,77 +252,82 @@ def tile_multilatentattention_pa_t_kernel(tc, x, Wqa, Wqb, out):
                 copy = nc.vector.tensor_copy if j == 1 else nc.scalar.copy
                 copy(out=cq_grouped[r][:, j], in_=cq_ps[:].rearrange("p t n -> p n t"))
 
-        def quantise_cq(r, half):
-            if half == 0:
-                codes = work.tile([P, TILES, P], U32, name="cq_codes", align_bytes=64)
-                scales = work.tile([P, TILES, P], U8, name="cq_scales", align_bytes=64)
+        def quantise_cq(r, j0, j1):
+            if j0 == 0:
+                codes = work.tile([P, TILES, P], U32, name="cq_codes", bufs=2, align_bytes=64)
+                scales = work.tile([P, TILES, P], U8, name="cq_scales", bufs=2, align_bytes=64)
                 cq_quantised[r] = (codes, scales)
             codes, scales = cq_quantised[r]
-            two = slice(2 * half, 2 * half + 2)
             nc.vector.quantize_mx(
-                out=codes[:, two].rearrange("p j n -> p (j n)").bitcast(FP8X4),
-                scales=scales[:, two].rearrange("p j n -> p (j n)"),
-                in_=cq_grouped[r][:, two].rearrange("p j n t -> p (j n t)"),
+                out=codes[:, j0:j1].rearrange("p j n -> p (j n)").bitcast(FP8X4),
+                scales=scales[:, j0:j1].rearrange("p j n -> p (j n)"),
+                in_=cq_grouped[r][:, j0:j1].rearrange("p j n t -> p (j n t)"),
             )
 
-        def second_product(r, half):
+        def second_product(r, j0, j1):
             codes, scales = cq_quantised[r]
-            o_sb = work.tile([P, HEADS, PAIR, HEAD], F32, name="o_sb", bufs=8)
-            plain_ps = next_bank([P, PAIR, PLAIN_COLS])
-            turned_ps = next_bank([P, PAIR, TURNED_COLS])
-            results[r, half] = (turned_ps, o_sb)
-            for jj in range(PAIR):
-                j = 2 * half + jj
-                for bank, cols in (
-                    (plain_ps, slice(0, PLAIN_COLS)),
-                    (turned_ps, slice(PLAIN_COLS, PLAIN_COLS + TURNED_COLS)),
-                ):
-                    nc.tensor.matmul_mx(
-                        out=bank[:, jj, :],
-                        lhsT=codes[:, j, :].bitcast(FP8X4),
-                        lhsT_scale=scales[:, j, :],
-                        rhs=wb_codes[:, cols].bitcast(FP8X4),
-                        rhs_scale=wb_scales[:, cols],
-                        start=True,
-                        stop=True,
-                    )
-            nc.scalar.copy(
-                out=o_sb[:, :, :, 0:NOPE].rearrange("p h j f -> p j h f"),
-                in_=plain_ps[:].rearrange("p j (h f) -> p j h f", f=NOPE),
-            )
+            if j0 == 0:
+                o_sb = work.tile([P, HEADS, TILES, HEAD], F32, name="o_sb", bufs=4)
+                results[r] = o_sb
+            o_sb = results[r]
+            turned_ps = None
+            for first in range(j0, j1, PAIR):
+                plain_ps = next_bank([P, PAIR, PLAIN_COLS])
+                if first == j0:
+                    turned_ps = next_bank([P, j1 - j0, TURNED_COLS])
+                    results[r, j0] = turned_ps
+                for j in range(first, first + PAIR):
+                    for place, cols in (
+                        (plain_ps[:, j - first, :], slice(0, PLAIN_COLS)),
+                        (turned_ps[:, j - j0, :], slice(PLAIN_COLS, PLAIN_COLS + TURNED_COLS)),
+                    ):
+                        nc.tensor.matmul_mx(
+                            out=place,
+                            lhsT=codes[:, j, :].bitcast(FP8X4),
+                            lhsT_scale=scales[:, j, :],
+                            rhs=wb_codes[:, cols].bitcast(FP8X4),
+                            rhs_scale=wb_scales[:, cols],
+                            start=True,
+                            stop=True,
+                        )
+                nc.scalar.copy(
+                    out=o_sb[:, :, first : first + PAIR, 0:NOPE].rearrange("p h j f -> p j h f"),
+                    in_=plain_ps[:].rearrange("p j (h f) -> p j h f", f=NOPE),
+                )
 
-        def rotate(r, half):
-            turned_ps, o_sb = results[r, half]
-            products = work.tile([P, PAIR, 2, TURNED_COLS], F32, name="products")
-            c = (r % ROUNDS_PER_SEQ) * TILES + 2 * half
-            results[r, half] = (products, o_sb)
+        def rotate(r, j0, j1):
+            turned_ps = results[r, j0]
+            tiles = j1 - j0
+            products = work.tile([P, 2, tiles, TURNED_COLS], F32, name="products", tag="products%d" % tiles, bufs=2)
+            results[r, j0] = products
+            c = (r % ROUNDS_PER_SEQ) * TILES + j0
             rotated = turned_ps[:].rearrange("p j (h i e) -> p j h i e", h=HEADS, e=2)
             for s, source in ((0, rotated), (1, rotated[:, :, :, :, ::-1])):
                 nc.vector.tensor_tensor(
-                    out=products[:, :, s].rearrange("p j (h i e) -> p j h i e", h=HEADS, e=2),
+                    out=products[:, s].rearrange("p j (h i e) -> p j h i e", h=HEADS, e=2),
                     in0=source,
-                    in1=factors[:, c : c + 2, s].unsqueeze(2).to_broadcast([P, PAIR, HEADS, PAIRS, 2]),
+                    in1=factors[:, c : c + tiles, s].unsqueeze(2).to_broadcast([P, tiles, HEADS, PAIRS, 2]),
                     op=ALU.mult,
                 )
 
-        def finish(r, half):
-            products, o_sb = results[r, half]
+        def finish(r, j0, j1):
+            products, o_sb = results[r, j0], results[r]
             nc.vector.tensor_tensor(
-                out=o_sb[:, :, :, NOPE:HEAD].rearrange("p h j f -> p j h f"),
-                in0=products[:, :, 0].rearrange("p j (h f) -> p j h f", h=HEADS),
-                in1=products[:, :, 1].rearrange("p j (h f) -> p j h f", h=HEADS),
+                out=o_sb[:, :, j0:j1, NOPE:HEAD].rearrange("p h j f -> p j h f"),
+                in0=products[:, 0].rearrange("p j (h f) -> p j h f", h=HEADS),
+                in1=products[:, 1].rearrange("p j (h f) -> p j h f", h=HEADS),
                 op=ALU.add,
             )
             b = r // ROUNDS_PER_SEQ
             n0 = (r % ROUNDS_PER_SEQ) * ROUND
-            two = slice(2 * half, 2 * half + 2)
             nc.sync.dma_start(
-                out=out[b, :, n0 : n0 + ROUND, :].rearrange("h (p j) f -> p h j f", j=TILES)[:, :, two, :],
-                in_=o_sb[:],
+                out=out[b, :, n0 : n0 + ROUND, :].rearrange("h (p j) f -> p h j f", j=TILES)[:, :, j0:j1, :],
+                in_=o_sb[:, :, j0:j1, :],
             )
 
-        sort_x(0, 0)
-        transpose_x(0, 0)
+        LAST = ROUNDS - 1
+        sort_x(0, 0, 2)
+        transpose_x(0, 0, 2)
         regroup_wa(nc.vector.tensor_copy, 0, 0)
         regroup_wa(nc.vector.tensor_copy, 0, 1)
         quantise_wa(0, 0)
@@ -331,47 +336,47 @@ def tile_multilatentattention_pa_t_kernel(tc, x, Wqa, Wqb, out):
         regroup_wa(nc.vector.tensor_copy, 1, 0)
         quantise_wa(1, 0)
         quantise_wa(1, 1)
-        quantise_x(0, 0)
-        sort_x(0, 1)
-        sort_x(1, 0)
+        quantise_x(0, 0, 2)
+        sort_x(0, 2, 4)
+        sort_x(1, 0, 2)
+        sort_x(1, 2, 4)
         regroup_wb()
+        first_product(0, 0, 2)
+        make_factors()
+        transpose_x(0, 2, 4)
+        quantise_x(0, 2, 4)
+        transpose_x(1, 0, 4)
+        sort_x(2, 0, 4)
+        quantise_wb()
+        quantise_x(1, 0, 4)
+        first_product(0, 2, 4)
+        quantise_cq(0, 0, 4)
 
-        for r in range(ROUNDS + 1):
-            here, ahead, sort, behind = r < ROUNDS, r + 1 < ROUNDS, r + 2 < ROUNDS, 0 <= r - 1
-            if behind:
-                rotate(r - 1, 0)
-                quantise_cq(r - 1, 1)
-                finish(r - 1, 0)
-            if here:
-                first_product(r, 0)
-            if behind:
-                second_product(r - 1, 1)
-                rotate(r - 1, 1)
-            if r == 0:
-                make_factors()
-                transpose_x(0, 1)
-                sort_x(1, 1)
-            elif sort:
-                sort_x(r + 2, 0)
-            if here:
-                quantise_cq(r, 0)
-            if r == 0:
-                quantise_x(0, 1)
-            if behind:
-                finish(r - 1, 1)
-            if ahead:
-                transpose_x(r + 1, 0)
-                transpose_x(r + 1, 1)
-                quantise_x(r + 1, 0)
-            if r == 0:
-                quantise_wb()
-            elif sort:
-                sort_x(r + 2, 1)
-            if ahead:
-                quantise_x(r + 1, 1)
-            if r == 0:
-                for half in range(2):
-                    sort_x(2, half)
-            if here:
-                first_product(r, 1)
-                second_product(r, 0)
+        for r in range(1, ROUNDS - 1):
+            if r >= 2:
+                rotate(r - 2, 0, 4)
+            transpose_x(r + 1, 0, 4)
+            if r + 2 < ROUNDS:
+                sort_x(r + 2, 0, 4)
+            if r >= 2:
+                finish(r - 2, 0, 4)
+            quantise_x(r + 1, 0, 4)
+            first_product(r, 0, 4)
+            quantise_cq(r, 0, 4)
+            second_product(r - 1, 0, 4)
+
+        rotate(LAST - 2, 0, 4)
+        first_product(LAST, 0, 2)
+        finish(LAST - 2, 0, 4)
+        quantise_cq(LAST, 0, 2)
+        first_product(LAST, 2, 4)
+        second_product(LAST - 1, 0, 4)
+        quantise_cq(LAST, 2, 4)
+        rotate(LAST - 1, 0, 4)
+        second_product(LAST, 0, 2)
+        finish(LAST - 1, 0, 4)
+        rotate(LAST, 0, 2)
+        second_product(LAST, 2, 4)
+        finish(LAST, 0, 2)
+        rotate(LAST, 2, 4)
+        finish(LAST, 2, 4)

@@ -51,6 +51,7 @@ def tile_multilatentattention_pa_t_kernel(tc, x, Wqa, Wqb, out):
 
         x_rounds = x.flatten_outer_dims().rearrange("(r p j) e -> r p j e", p=P, j=TILES)
         x_sb = keep.tile([P, ROUNDS, TILES, EMB], BF16)
+        x_words = x_sb[:].bitcast(F32)
         wa_raw = keep.tile([P, PASSES_1, PACK, RANK], BF16)
         wb_raw = keep.tile([P, PACK, HEADS * HEAD], BF16)
 
@@ -58,12 +59,10 @@ def tile_multilatentattention_pa_t_kernel(tc, x, Wqa, Wqb, out):
             nc.sync.dma_start(out=x_sb[:, r, j : j + count, :], in_=x_rounds[r][:, j : j + count, :])
 
         def load_wa(g):
-            rows = Wqa.rearrange("(g q u i e) c -> g i q u (e c)", g=PASSES_1, u=2, i=2, e=2)
-            for i in range(2):
-                nc.sync.dma_start(
-                    out=wa_raw[i::2, g].rearrange("p (u e) c -> p u (e c)", e=2),
-                    in_=rows[g, i],
-                )
+            nc.sync.dma_start(
+                out=wa_raw[:, g].rearrange("p t c -> p (t c)"),
+                in_=Wqa.rearrange("(g p t) c -> g p (t c)", p=P, t=PACK)[g],
+            )
 
         load_x(0, 0, 2)
         load_wa(0)
@@ -138,7 +137,6 @@ def tile_multilatentattention_pa_t_kernel(tc, x, Wqa, Wqb, out):
         wa_grouped = keep.tile([P, PASSES_1, RANK, PACK], BF16, align_bytes=64)
         wa_codes = keep.tile([P, PASSES_1, RANK], U32, align_bytes=64)
         wa_scales = keep.tile([P, PASSES_1, RANK], U8, align_bytes=64)
-        HALF = RANK // 2
 
         def copy_on_gpsimd(out, in_):
             nc.gpsimd.tensor_scalar(out=out, in0=in_, scalar1=1.0, scalar2=0.0, op0=ALU.mult, op1=ALU.add)
@@ -149,12 +147,11 @@ def tile_multilatentattention_pa_t_kernel(tc, x, Wqa, Wqb, out):
                 in_=wa_raw[:, g].rearrange("p j (q t i) -> p t q j i", t=RANK_TILES, i=4)[:, 2 * half : 2 * half + 2],
             )
 
-        def quantise_wa(g, half):
-            cols = slice(half * HALF, (half + 1) * HALF)
+        def quantise_wa(g):
             nc.vector.quantize_mx(
-                out=wa_codes[:, g, cols].bitcast(FP8X4),
-                scales=wa_scales[:, g, cols],
-                in_=wa_grouped[:, g, cols].rearrange("p c t -> p (c t)"),
+                out=wa_codes[:, g].bitcast(FP8X4),
+                scales=wa_scales[:, g],
+                in_=wa_grouped[:, g].rearrange("p c t -> p (c t)"),
             )
 
         wb_codes = keep.tile([P, PLAIN_COLS + TURNED_COLS], U32, align_bytes=64)
@@ -189,31 +186,23 @@ def tile_multilatentattention_pa_t_kernel(tc, x, Wqa, Wqb, out):
             banks_taken.append(tag)
             return bank
 
-        x_sorted = {}
         x_grouped, x_quantised = {}, {}
         cq_grouped, cq_quantised = {}, {}
         results = {}
-
-        def sort_x(r, j0, j1):
-            sorted_x = work.tile([P, 2, j1 - j0, WORDS], BF16, name="x_sorted", tag="x_sorted%d" % (j1 - j0), bufs=2)
-            for j in range(j0, j1):
-                x_sorted[r, j] = (sorted_x, j - j0)
-            nc.vector.tensor_copy(
-                out=sorted_x[:].rearrange("p u j (q i) -> p u j q i", i=4),
-                in_=x_sb[:, r, j0:j1, :].rearrange("p j (q u i) -> p u j q i", u=2, i=4),
-            )
 
         def transpose_x(r, j0, j1):
             if j0 == 0:
                 grouped = work.tile([P, TILES, PASSES_1, P, PACK], BF16, name="x_grouped", bufs=2, align_bytes=64)
                 x_grouped[r] = grouped
             for j in range(j0, j1):
-                sorted_x, place = x_sorted[r, j]
-                words = sorted_x[:].bitcast(F32)
                 xt = next_bank([P, PASSES_1 * 2, P])
                 for g in range(PASSES_1):
                     for u in range(2):
-                        nc.tensor.transpose(xt[:, 2 * g + u, :], words[:, u, place, g * P : (g + 1) * P], ident[:])
+                        nc.tensor.transpose(
+                            xt[:, 2 * g + u, :],
+                            x_words[:, r, j, 2 * g * P + u : 2 * (g + 1) * P : 2],
+                            ident[:],
+                        )
                 nc.scalar.copy(
                     out=x_grouped[r][:, j].bitcast(F32),
                     in_=xt[:].rearrange("p (g u) n -> p g n u", u=2),
@@ -249,7 +238,7 @@ def tile_multilatentattention_pa_t_kernel(tc, x, Wqa, Wqb, out):
                             start=(g == 0),
                             stop=(g == PASSES_1 - 1),
                         )
-                copy = nc.vector.tensor_copy if j == 1 else nc.scalar.copy
+                copy = nc.vector.tensor_copy if j % 2 == 1 else nc.scalar.copy
                 copy(out=cq_grouped[r][:, j], in_=cq_ps[:].rearrange("p t n -> p n t"))
 
         def quantise_cq(r, j0, j1):
@@ -310,9 +299,9 @@ def tile_multilatentattention_pa_t_kernel(tc, x, Wqa, Wqb, out):
                     op=ALU.mult,
                 )
 
-        def finish(r, j0, j1):
+        def finish(engine, r, j0, j1):
             products, o_sb = results[r, j0], results[r]
-            nc.vector.tensor_tensor(
+            engine.tensor_tensor(
                 out=o_sb[:, :, j0:j1, NOPE:HEAD].rearrange("p h j f -> p j h f"),
                 in0=products[:, 0].rearrange("p j (h f) -> p j h f", h=HEADS),
                 in1=products[:, 1].rearrange("p j (h f) -> p j h f", h=HEADS),
@@ -326,57 +315,49 @@ def tile_multilatentattention_pa_t_kernel(tc, x, Wqa, Wqb, out):
             )
 
         LAST = ROUNDS - 1
-        sort_x(0, 0, 2)
         transpose_x(0, 0, 2)
         regroup_wa(nc.vector.tensor_copy, 0, 0)
-        regroup_wa(nc.vector.tensor_copy, 0, 1)
-        quantise_wa(0, 0)
-        quantise_wa(0, 1)
+        regroup_wa(nc.scalar.copy, 0, 1)
+        quantise_x(0, 0, 2)
         regroup_wa(nc.scalar.copy, 1, 1)
         regroup_wa(nc.vector.tensor_copy, 1, 0)
-        quantise_wa(1, 0)
-        quantise_wa(1, 1)
-        quantise_x(0, 0, 2)
-        sort_x(0, 2, 4)
-        sort_x(1, 0, 2)
-        sort_x(1, 2, 4)
+        quantise_wa(0)
+        quantise_wa(1)
+        transpose_x(0, 2, 4)
         regroup_wb()
         first_product(0, 0, 2)
-        make_factors()
-        transpose_x(0, 2, 4)
         quantise_x(0, 2, 4)
+        make_factors()
         transpose_x(1, 0, 4)
-        sort_x(2, 0, 4)
+        quantise_cq(0, 0, 2)
         quantise_wb()
-        quantise_x(1, 0, 4)
+        quantise_x(1, 0, 2)
+        quantise_x(1, 2, 4)
         first_product(0, 2, 4)
-        quantise_cq(0, 0, 4)
 
         for r in range(1, ROUNDS - 1):
-            if r >= 2:
-                rotate(r - 2, 0, 4)
+            quantise_cq(r - 1, 2, 4)
             transpose_x(r + 1, 0, 4)
-            if r + 2 < ROUNDS:
-                sort_x(r + 2, 0, 4)
-            if r >= 2:
-                finish(r - 2, 0, 4)
-            quantise_x(r + 1, 0, 4)
-            first_product(r, 0, 4)
-            quantise_cq(r, 0, 4)
+            quantise_x(r + 1, 0, 2)
+            quantise_x(r + 1, 2, 4)
             second_product(r - 1, 0, 4)
+            rotate(r - 1, 0, 4)
+            finish(nc.gpsimd, r - 1, 0, 4)
+            first_product(r, 0, 2)
+            quantise_cq(r, 0, 2)
+            first_product(r, 2, 4)
 
-        rotate(LAST - 2, 0, 4)
+        quantise_cq(LAST - 1, 2, 4)
         first_product(LAST, 0, 2)
-        finish(LAST - 2, 0, 4)
         quantise_cq(LAST, 0, 2)
-        first_product(LAST, 2, 4)
         second_product(LAST - 1, 0, 4)
-        quantise_cq(LAST, 2, 4)
+        first_product(LAST, 2, 4)
         rotate(LAST - 1, 0, 4)
+        finish(nc.gpsimd, LAST - 1, 0, 4)
         second_product(LAST, 0, 2)
-        finish(LAST - 1, 0, 4)
+        quantise_cq(LAST, 2, 4)
         rotate(LAST, 0, 2)
+        finish(nc.vector, LAST, 0, 2)
         second_product(LAST, 2, 4)
-        finish(LAST, 0, 2)
         rotate(LAST, 2, 4)
-        finish(LAST, 2, 4)
+        finish(nc.vector, LAST, 2, 4)

@@ -64,9 +64,10 @@ def tile_multilatentattention_pa_t_kernel(tc, x, Wqa, Wqb, out):
                 in_=Wqa.rearrange("(g p t) c -> g p (t c)", p=P, t=PACK)[g],
             )
 
-        load_x(0, 0, 2)
         load_wa(0)
         load_wa(1)
+        load_x(0, 0, 1)
+        load_x(0, 1, 1)
         load_x(0, 2, 2)
         load_x(1, 0, 2)
         load_x(1, 2, 2)
@@ -220,7 +221,7 @@ def tile_multilatentattention_pa_t_kernel(tc, x, Wqa, Wqb, out):
                 in_=x_grouped[r][:, j0:j1].rearrange("p j g n t -> p (j g n t)"),
             )
 
-        def first_product(r, j0, j1):
+        def first_product(r, j0, j1, vector_tiles):
             codes, scales = x_quantised[r]
             if j0 == 0:
                 grouped = work.tile([P, TILES, P, PACK], BF16, name="cq_grouped", bufs=2, align_bytes=64)
@@ -238,7 +239,7 @@ def tile_multilatentattention_pa_t_kernel(tc, x, Wqa, Wqb, out):
                             start=(g == 0),
                             stop=(g == PASSES_1 - 1),
                         )
-                copy = nc.vector.tensor_copy if j % 2 == 1 else nc.scalar.copy
+                copy = nc.vector.tensor_copy if j in vector_tiles else nc.scalar.copy
                 copy(out=cq_grouped[r][:, j], in_=cq_ps[:].rearrange("p t n -> p n t"))
 
         def quantise_cq(r, j0, j1):
@@ -299,8 +300,9 @@ def tile_multilatentattention_pa_t_kernel(tc, x, Wqa, Wqb, out):
                     op=ALU.mult,
                 )
 
-        def finish(engine, r, j0, j1):
+        def finish(r, j0, j1):
             products, o_sb = results[r, j0], results[r]
+            engine = nc.gpsimd if r == ROUNDS - 2 else nc.vector
             engine.tensor_tensor(
                 out=o_sb[:, :, j0:j1, NOPE:HEAD].rearrange("p h j f -> p j h f"),
                 in0=products[:, 0].rearrange("p j (h f) -> p j h f", h=HEADS),
@@ -315,17 +317,18 @@ def tile_multilatentattention_pa_t_kernel(tc, x, Wqa, Wqb, out):
             )
 
         LAST = ROUNDS - 1
-        transpose_x(0, 0, 2)
         regroup_wa(nc.vector.tensor_copy, 0, 0)
-        regroup_wa(nc.scalar.copy, 0, 1)
-        quantise_x(0, 0, 2)
+        regroup_wa(nc.vector.tensor_copy, 0, 1)
+        quantise_wa(0)
         regroup_wa(nc.scalar.copy, 1, 1)
         regroup_wa(nc.vector.tensor_copy, 1, 0)
-        quantise_wa(0)
         quantise_wa(1)
+        transpose_x(0, 0, 2)
+        quantise_x(0, 0, 1)
+        quantise_x(0, 1, 2)
         transpose_x(0, 2, 4)
         regroup_wb()
-        first_product(0, 0, 2)
+        first_product(0, 0, 2, (1,))
         quantise_x(0, 2, 4)
         make_factors()
         transpose_x(1, 0, 4)
@@ -333,31 +336,37 @@ def tile_multilatentattention_pa_t_kernel(tc, x, Wqa, Wqb, out):
         quantise_wb()
         quantise_x(1, 0, 2)
         quantise_x(1, 2, 4)
-        first_product(0, 2, 4)
+        first_product(0, 2, 4, (3,))
 
-        for r in range(1, ROUNDS - 1):
+        for r in range(1, LAST):
             quantise_cq(r - 1, 2, 4)
+            if r >= 2:
+                finish(r - 2, 0, 4)
             transpose_x(r + 1, 0, 4)
             quantise_x(r + 1, 0, 2)
             quantise_x(r + 1, 2, 4)
             second_product(r - 1, 0, 4)
             rotate(r - 1, 0, 4)
-            finish(nc.gpsimd, r - 1, 0, 4)
-            first_product(r, 0, 2)
+            first_product(r, 0, 2, (1,) if r % 2 == 0 and r < LAST - 1 else ())
             quantise_cq(r, 0, 2)
-            first_product(r, 2, 4)
+            first_product(r, 2, 4, (3,))
 
-        quantise_cq(LAST - 1, 2, 4)
-        first_product(LAST, 0, 2)
+        r = LAST - 1
+        quantise_cq(r, 2, 4)
+        first_product(LAST, 0, 2, ())
+        second_product(r, 0, 2)
+        finish(r - 1, 0, 4)
+        rotate(r, 0, 2)
         quantise_cq(LAST, 0, 2)
-        second_product(LAST - 1, 0, 4)
-        first_product(LAST, 2, 4)
-        rotate(LAST - 1, 0, 4)
-        finish(nc.gpsimd, LAST - 1, 0, 4)
-        second_product(LAST, 0, 2)
+        first_product(LAST, 2, 4, (3,))
         quantise_cq(LAST, 2, 4)
+        second_product(r, 2, 4)
+        rotate(r, 2, 4)
+        second_product(LAST, 0, 2)
+        finish(r, 0, 2)
         rotate(LAST, 0, 2)
-        finish(nc.vector, LAST, 0, 2)
         second_product(LAST, 2, 4)
+        finish(r, 2, 4)
         rotate(LAST, 2, 4)
-        finish(nc.vector, LAST, 2, 4)
+        finish(LAST, 0, 2)
+        finish(LAST, 2, 4)

@@ -66,9 +66,8 @@ def tile_multilatentattention_pa_t_kernel(tc, x, Wqa, Wqb, out):
 
         load_wa(0)
         load_wa(1)
-        load_x(0, 0, 1)
-        load_x(0, 1, 1)
-        load_x(0, 2, 2)
+        for j in range(TILES):
+            load_x(0, j, 1)
         load_x(1, 0, 2)
         load_x(1, 2, 2)
         rows = Wqb.rearrange("(q t i) n -> i q t n", t=PACK, i=4)
@@ -191,7 +190,7 @@ def tile_multilatentattention_pa_t_kernel(tc, x, Wqa, Wqb, out):
         cq_grouped, cq_quantised = {}, {}
         results = {}
 
-        def transpose_x(r, j0, j1):
+        def transpose_x(r, j0, j1, vector_tiles=()):
             if j0 == 0:
                 grouped = work.tile([P, TILES, PASSES_1, P, PACK], BF16, name="x_grouped", bufs=2, align_bytes=64)
                 x_grouped[r] = grouped
@@ -204,7 +203,8 @@ def tile_multilatentattention_pa_t_kernel(tc, x, Wqa, Wqb, out):
                             x_words[:, r, j, 2 * g * P + u : 2 * (g + 1) * P : 2],
                             ident[:],
                         )
-                nc.scalar.copy(
+                copy = nc.vector.tensor_copy if j in vector_tiles else nc.scalar.copy
+                copy(
                     out=x_grouped[r][:, j].bitcast(F32),
                     in_=xt[:].rearrange("p (g u) n -> p g n u", u=2),
                 )
@@ -288,7 +288,7 @@ def tile_multilatentattention_pa_t_kernel(tc, x, Wqa, Wqb, out):
         def rotate(r, j0, j1):
             turned_ps = results[r, j0]
             tiles = j1 - j0
-            products = work.tile([P, 2, tiles, TURNED_COLS], F32, name="products", tag="products%d" % tiles, bufs=2)
+            products = work.tile([P, 2, tiles, TURNED_COLS], F32, name="products", tag="products%d" % tiles, bufs=8 // tiles)
             results[r, j0] = products
             c = (r % ROUNDS_PER_SEQ) * TILES + j0
             rotated = turned_ps[:].rearrange("p j (h i e) -> p j h i e", h=HEADS, e=2)
@@ -302,7 +302,7 @@ def tile_multilatentattention_pa_t_kernel(tc, x, Wqa, Wqb, out):
 
         def finish(r, j0, j1):
             products, o_sb = results[r, j0], results[r]
-            engine = nc.gpsimd if r == ROUNDS - 2 else nc.vector
+            engine = nc.gpsimd if j1 - j0 == PAIR and (r, j0) != (ROUNDS - 1, PAIR) else nc.vector
             engine.tensor_tensor(
                 out=o_sb[:, :, j0:j1, NOPE:HEAD].rearrange("p h j f -> p j h f"),
                 in0=products[:, 0].rearrange("p j (h f) -> p j h f", h=HEADS),
@@ -340,14 +340,14 @@ def tile_multilatentattention_pa_t_kernel(tc, x, Wqa, Wqb, out):
 
         for r in range(1, LAST):
             quantise_cq(r - 1, 2, 4)
+            transpose_x(r + 1, 0, 4, (0,))
             if r >= 2:
                 finish(r - 2, 0, 4)
-            transpose_x(r + 1, 0, 4)
             quantise_x(r + 1, 0, 2)
             quantise_x(r + 1, 2, 4)
             second_product(r - 1, 0, 4)
             rotate(r - 1, 0, 4)
-            first_product(r, 0, 2, (1,) if r % 2 == 0 and r < LAST - 1 else ())
+            first_product(r, 0, 2, ())
             quantise_cq(r, 0, 2)
             first_product(r, 2, 4, (3,))
 
@@ -358,15 +358,15 @@ def tile_multilatentattention_pa_t_kernel(tc, x, Wqa, Wqb, out):
         finish(r - 1, 0, 4)
         rotate(r, 0, 2)
         quantise_cq(LAST, 0, 2)
-        first_product(LAST, 2, 4, (3,))
-        quantise_cq(LAST, 2, 4)
+        first_product(LAST, 2, 4, ())
         second_product(r, 2, 4)
-        rotate(r, 2, 4)
-        second_product(LAST, 0, 2)
         finish(r, 0, 2)
-        rotate(LAST, 0, 2)
-        second_product(LAST, 2, 4)
+        rotate(r, 2, 4)
+        quantise_cq(LAST, 2, 4)
         finish(r, 2, 4)
-        rotate(LAST, 2, 4)
+        second_product(LAST, 0, 2)
+        rotate(LAST, 0, 2)
         finish(LAST, 0, 2)
+        second_product(LAST, 2, 4)
+        rotate(LAST, 2, 4)
         finish(LAST, 2, 4)

import math
from contextlib import ExitStack

import concourse.mybir as mybir
from concourse.masks import make_identity

F32 = mybir.dt.float32
BF16 = mybir.dt.bfloat16
I32 = mybir.dt.int32
U32 = mybir.dt.uint32
U8 = mybir.dt.uint8
FP8X4 = mybir.dt.float8_e4m3fn_x4
ALU = mybir.AluOpType
ACT = mybir.ActivationFunctionType

P = 128
PACK = 4
BATCH, SEQ, EMB = 4, 1024, 1024
HEADS, NOPE, ROPE = 4, 64, 32
HEAD = NOPE + ROPE
RANK = 512
PAIRS = ROPE // 2
BASE = 10000.0

TILES = 4
ROUND = TILES * P
ROUNDS_PER_SEQ = SEQ // ROUND
ROUNDS = BATCH * SEQ // ROUND
PAIR = 2
PASSES_1 = EMB // (P * PACK)
RANK_TILES = RANK // P
BANKS = 8
WORDS = EMB // 2
PLAIN_COLS = HEADS * NOPE
TURNED_COLS = HEADS * ROPE

FLOPS = 2 * BATCH * SEQ * (EMB * RANK + RANK * HEADS * HEAD)

TWO_PI = 2.0 * math.pi
TWO_PI_HIGH = math.floor(TWO_PI * 8192.0) / 8192.0
TWO_PI_LOW = TWO_PI - TWO_PI_HIGH


def tile_multilatentattention_pa_t_kernel(tc, x, Wqa, Wqb, out):
    nc = tc.nc
    with ExitStack() as ctx:
        keep = ctx.enter_context(tc.tile_pool(name="keep", bufs=1))
        work = ctx.enter_context(tc.tile_pool(name="work", bufs=3))
        psum = ctx.enter_context(tc.psum_pool(name="psum", bufs=1))
        ctx.enter_context(tc.manual_schedule())

        x_rounds = x.flatten_outer_dims().rearrange("(r p j) e -> r p j e", p=P, j=TILES)
        x_sb = keep.tile([P, ROUNDS, TILES, EMB], BF16)
        x_words = x_sb[:].bitcast(F32)
        wa_raw = keep.tile([P, PASSES_1, PACK, RANK], BF16)
        wb_raw = keep.tile([P, PACK, HEADS * HEAD], BF16)

        def load_x(r, j, count):
            nc.sync.dma_start(out=x_sb[:, r, j : j + count, :], in_=x_rounds[r][:, j : j + count, :])

        def load_wa(g):
            nc.sync.dma_start(
                out=wa_raw[:, g].rearrange("p t c -> p (t c)"),
                in_=Wqa.rearrange("(g p t) c -> g p (t c)", p=P, t=PACK)[g],
            )

        load_wa(0)
        load_wa(1)
        for j in range(TILES):
            load_x(0, j, 1)
        load_x(1, 0, 2)
        load_x(1, 2, 2)
        rows = Wqb.rearrange("(q t i) n -> i q t n", t=PACK, i=4)
        for i in range(4):
            nc.sync.dma_start(out=wb_raw[i::4], in_=rows[i])
        for r in range(2, ROUNDS):
            load_x(r, 0, TILES)

        zero = keep.tile([P, 1], F32)
        nc.gpsimd.memset(zero[:], 0.0)
        warm = keep.tile([P, 1], F32)
        nc.scalar.activation(out=warm[:], in_=zero[:], func=ACT.Sin)

        classes = ROUNDS_PER_SEQ * TILES
        position = keep.tile([P, classes], F32)
        nc.gpsimd.iota(
            position[:],
            pattern=[[ROUND, ROUNDS_PER_SEQ], [1, TILES]],
            base=0,
            channel_multiplier=TILES,
            allow_small_or_imprecise_dtypes=True,
        )
        ident = keep.tile([P, P], F32)
        make_identity(nc, ident[:])

        angle = keep.tile([P, classes, PAIRS], F32)
        for i in range(PAIRS):
            nc.vector.tensor_scalar(
                out=angle[:, :, i],
                in0=position[:],
                scalar1=BASE ** (-float(i) / PAIRS),
                scalar2=None,
                op0=ALU.mult,
            )
        turns_int = keep.tile([P, classes, PAIRS], I32)
        nc.vector.tensor_scalar(out=turns_int[:], in0=angle[:], scalar1=1.0 / TWO_PI, scalar2=None, op0=ALU.mult)
        turns = keep.tile([P, classes, PAIRS], F32)
        nc.vector.tensor_copy(out=turns[:], in_=turns_int[:])
        wrap = keep.tile([P, classes, PAIRS], F32)

        def add_multiple(values, factor, op0, scalar2):
            if scalar2 is None:
                nc.gpsimd.tensor_scalar(out=wrap[:], in0=values[:], scalar1=factor, scalar2=0.0, op0=ALU.mult, op1=ALU.add)
            else:
                nc.gpsimd.tensor_scalar(out=wrap[:], in0=values[:], scalar1=factor, scalar2=scalar2, op0=op0, op1=ALU.mult)
            nc.gpsimd.tensor_tensor(out=angle[:], in0=angle[:], in1=wrap[:], op=ALU.add)

        add_multiple(turns, -TWO_PI_HIGH, ALU.mult, None)
        add_multiple(turns, -TWO_PI_LOW, ALU.mult, None)
        add_multiple(angle, math.pi, ALU.is_gt, -TWO_PI)
        add_multiple(angle, -math.pi, ALU.is_lt, TWO_PI)
        size = keep.tile([P, classes, PAIRS], F32)
        factors = keep.tile([P, classes, 2, PAIRS, 2], F32)

        def make_factors():
            nc.scalar.activation(out=size[:], in_=angle[:], func=ACT.Abs)
            nc.scalar.activation(
                out=factors[:, :, 0],
                in_=size[:].unsqueeze(3).to_broadcast([P, classes, PAIRS, 2]),
                func=ACT.Sin,
                scale=-1.0,
                bias=0.5 * math.pi,
            )
            for e, sign in ((0, -1.0), (1, 1.0)):
                nc.scalar.activation(out=factors[:, :, 1, :, e], in_=angle[:], func=ACT.Sin, scale=sign)

        wa_grouped = keep.tile([P, PASSES_1, RANK, PACK], BF16, align_bytes=64)
        wa_codes = keep.tile([P, PASSES_1, RANK], U32, align_bytes=64)
        wa_scales = keep.tile([P, PASSES_1, RANK], U8, align_bytes=64)

        def copy_on_gpsimd(out, in_):
            nc.gpsimd.tensor_scalar(out=out, in0=in_, scalar1=1.0, scalar2=0.0, op0=ALU.mult, op1=ALU.add)

        def regroup_wa(copy, g, half):
            copy(
                out=wa_grouped[:, g].rearrange("p (t q i) j -> p t q j i", t=RANK_TILES, i=4)[:, 2 * half : 2 * half + 2],
                in_=wa_raw[:, g].rearrange("p j (q t i) -> p t q j i", t=RANK_TILES, i=4)[:, 2 * half : 2 * half + 2],
            )

        def quantise_wa(g):
            nc.vector.quantize_mx(
                out=wa_codes[:, g].bitcast(FP8X4),
                scales=wa_scales[:, g],
                in_=wa_grouped[:, g].rearrange("p c t -> p (c t)"),
            )

        wb_codes = keep.tile([P, PLAIN_COLS + TURNED_COLS], U32, align_bytes=64)
        wb_scales = keep.tile([P, PLAIN_COLS + TURNED_COLS], U8, align_bytes=64)

        wb_grouped = keep.tile([P, PLAIN_COLS + TURNED_COLS, PACK], BF16, align_bytes=64)

        def regroup_wb():
            by_head = wb_raw[:].rearrange("p t (h f) -> p h f t", f=HEAD)
            copy_on_gpsimd(
                out=wb_grouped[:, 0:PLAIN_COLS, :].rearrange("p (h f) t -> p h f t", f=NOPE),
                in_=by_head[:, :, 0:NOPE, :],
            )
            copy_on_gpsimd(
                out=wb_grouped[:, PLAIN_COLS:, :].rearrange("p (h f) t -> p h f t", f=ROPE),
                in_=by_head[:, :, NOPE:HEAD, :],
            )

        def quantise_wb():
            for cols in (slice(0, PLAIN_COLS), slice(PLAIN_COLS, PLAIN_COLS + TURNED_COLS)):
                nc.vector.quantize_mx(
                    out=wb_codes[:, cols].bitcast(FP8X4),
                    scales=wb_scales[:, cols],
                    in_=wb_grouped[:, cols, :].rearrange("p c t -> p (c t)"),
                )

        banks_taken = []

        def next_bank(shape):
            tag = "bank%d" % (len(banks_taken) % BANKS)
            bank = psum.tile(shape, F32, name=tag, tag=tag)
            banks_taken.append(tag)
            return bank

        x_grouped, x_quantised = {}, {}
        cq_grouped, cq_quantised = {}, {}
        results = {}

        def transpose_x(r, j0, j1, vector_tiles=()):
            if j0 == 0:
                grouped = work.tile([P, TILES, PASSES_1, P, PACK], BF16, name="x_grouped", bufs=2, align_bytes=64)
                x_grouped[r] = grouped
            for j in range(j0, j1):
                xt = next_bank([P, PASSES_1 * 2, P])
                for g in range(PASSES_1):
                    for u in range(2):
                        nc.tensor.transpose(
                            xt[:, 2 * g + u, :],
                            x_words[:, r, j, 2 * g * P + u : 2 * (g + 1) * P : 2],
                            ident[:],
                        )
                copy = nc.vector.tensor_copy if j in vector_tiles else nc.scalar.copy
                copy(
                    out=x_grouped[r][:, j].bitcast(F32),
                    in_=xt[:].rearrange("p (g u) n -> p g n u", u=2),
                )

        def quantise_x(r, j0, j1):
            if j0 == 0:
                codes = work.tile([P, TILES, PASSES_1, P], U32, name="x_codes", bufs=2, align_bytes=64)
                scales = work.tile([P, TILES, PASSES_1, P], U8, name="x_scales", bufs=2, align_bytes=64)
                x_quantised[r] = (codes, scales)
            codes, scales = x_quantised[r]
            nc.vector.quantize_mx(
                out=codes[:, j0:j1].rearrange("p j g n -> p (j g n)").bitcast(FP8X4),
                scales=scales[:, j0:j1].rearrange("p j g n -> p (j g n)"),
                in_=x_grouped[r][:, j0:j1].rearrange("p j g n t -> p (j g n t)"),
            )

        def first_product(r, j0, j1, vector_tiles):
            codes, scales = x_quantised[r]
            if j0 == 0:
                grouped = work.tile([P, TILES, P, PACK], BF16, name="cq_grouped", bufs=2, align_bytes=64)
                cq_grouped[r] = grouped
            for j in range(j0, j1):
                cq_ps = next_bank([P, RANK_TILES, P])
                for t in range(RANK_TILES):
                    for g in range(PASSES_1):
                        nc.tensor.matmul_mx(
                            out=cq_ps[:, t, :],
                            lhsT=wa_codes[:, g, t * P : (t + 1) * P].bitcast(FP8X4),
                            lhsT_scale=wa_scales[:, g, t * P : (t + 1) * P],
                            rhs=codes[:, j, g, :].bitcast(FP8X4),
                            rhs_scale=scales[:, j, g, :],
                            start=(g == 0),
                            stop=(g == PASSES_1 - 1),
                        )
                copy = nc.vector.tensor_copy if j in vector_tiles else nc.scalar.copy
                copy(out=cq_grouped[r][:, j], in_=cq_ps[:].rearrange("p t n -> p n t"))

        def quantise_cq(r, j0, j1):
            if j0 == 0:
                codes = work.tile([P, TILES, P], U32, name="cq_codes", bufs=2, align_bytes=64)
                scales = work.tile([P, TILES, P], U8, name="cq_scales", bufs=2, align_bytes=64)
                cq_quantised[r] = (codes, scales)
            codes, scales = cq_quantised[r]
            nc.vector.quantize_mx(
                out=codes[:, j0:j1].rearrange("p j n -> p (j n)").bitcast(FP8X4),
                scales=scales[:, j0:j1].rearrange("p j n -> p (j n)"),
                in_=cq_grouped[r][:, j0:j1].rearrange("p j n t -> p (j n t)"),
            )

        def second_product(r, j0, j1):
            codes, scales = cq_quantised[r]
            if j0 == 0:
                o_sb = work.tile([P, HEADS, TILES, HEAD], F32, name="o_sb", bufs=4)
                results[r] = o_sb
            o_sb = results[r]
            turned_ps = None
            for first in range(j0, j1, PAIR):
                plain_ps = next_bank([P, PAIR, PLAIN_COLS])
                if first == j0:
                    turned_ps = next_bank([P, j1 - j0, TURNED_COLS])
                    results[r, j0] = turned_ps
                for j in range(first, first + PAIR):
                    for place, cols in (
                        (plain_ps[:, j - first, :], slice(0, PLAIN_COLS)),
                        (turned_ps[:, j - j0, :], slice(PLAIN_COLS, PLAIN_COLS + TURNED_COLS)),
                    ):
                        nc.tensor.matmul_mx(
                            out=place,
                            lhsT=codes[:, j, :].bitcast(FP8X4),
                            lhsT_scale=scales[:, j, :],
                            rhs=wb_codes[:, cols].bitcast(FP8X4),
                            rhs_scale=wb_scales[:, cols],
                            start=True,
                            stop=True,
                        )
                nc.scalar.copy(
                    out=o_sb[:, :, first : first + PAIR, 0:NOPE].rearrange("p h j f -> p j h f"),
                    in_=plain_ps[:].rearrange("p j (h f) -> p j h f", f=NOPE),
                )

        def rotate(r, j0, j1):
            turned_ps = results[r, j0]
            tiles = j1 - j0
            products = work.tile([P, 2, tiles, TURNED_COLS], F32, name="products", tag="products%d" % tiles, bufs=8 // tiles)
            results[r, j0] = products
            c = (r % ROUNDS_PER_SEQ) * TILES + j0
            rotated = turned_ps[:].rearrange("p j (h i e) -> p j h i e", h=HEADS, e=2)
            for s, source in ((0, rotated), (1, rotated[:, :, :, :, ::-1])):
                nc.vector.tensor_tensor(
                    out=products[:, s].rearrange("p j (h i e) -> p j h i e", h=HEADS, e=2),
                    in0=source,
                    in1=factors[:, c : c + tiles, s].unsqueeze(2).to_broadcast([P, tiles, HEADS, PAIRS, 2]),
                    op=ALU.mult,
                )

        def finish(r, j0, j1):
            products, o_sb = results[r, j0], results[r]
            engine = nc.gpsimd if j1 - j0 == PAIR and (r, j0) != (ROUNDS - 1, PAIR) else nc.vector
            engine.tensor_tensor(
                out=o_sb[:, :, j0:j1, NOPE:HEAD].rearrange("p h j f -> p j h f"),
                in0=products[:, 0].rearrange("p j (h f) -> p j h f", h=HEADS),
                in1=products[:, 1].rearrange("p j (h f) -> p j h f", h=HEADS),
                op=ALU.add,
            )
            b = r // ROUNDS_PER_SEQ
            n0 = (r % ROUNDS_PER_SEQ) * ROUND
            nc.sync.dma_start(
                out=out[b, :, n0 : n0 + ROUND, :].rearrange("h (p j) f -> p h j f", j=TILES)[:, :, j0:j1, :],
                in_=o_sb[:, :, j0:j1, :],
            )

        LAST = ROUNDS - 1
        regroup_wa(nc.vector.tensor_copy, 0, 0)
        regroup_wa(nc.vector.tensor_copy, 0, 1)
        quantise_wa(0)
        regroup_wa(nc.scalar.copy, 1, 1)
        regroup_wa(nc.vector.tensor_copy, 1, 0)
        quantise_wa(1)
        transpose_x(0, 0, 2)
        quantise_x(0, 0, 1)
        quantise_x(0, 1, 2)
        transpose_x(0, 2, 4)
        regroup_wb()
        first_product(0, 0, 2, (1,))
        quantise_x(0, 2, 4)
        make_factors()
        transpose_x(1, 0, 4)
        quantise_cq(0, 0, 2)
        quantise_wb()
        quantise_x(1, 0, 2)
        quantise_x(1, 2, 4)
        first_product(0, 2, 4, (3,))

        for r in range(1, LAST):
            quantise_cq(r - 1, 2, 4)
            transpose_x(r + 1, 0, 4, (0,))
            if r >= 2:
                finish(r - 2, 0, 4)
            quantise_x(r + 1, 0, 2)
            quantise_x(r + 1, 2, 4)
            second_product(r - 1, 0, 4)
            rotate(r - 1, 0, 4)
            first_product(r, 0, 2, ())
            quantise_cq(r, 0, 2)
            first_product(r, 2, 4, (3,))

        r = LAST - 1
        quantise_cq(r, 2, 4)
        first_product(LAST, 0, 2, ())
        second_product(r, 0, 2)
        finish(r - 1, 0, 4)
        rotate(r, 0, 2)
        quantise_cq(LAST, 0, 2)
        first_product(LAST, 2, 4, ())
        second_product(r, 2, 4)
        finish(r, 0, 2)
        rotate(r, 2, 4)
        quantise_cq(LAST, 2, 4)
        finish(r, 2, 4)
        second_product(LAST, 0, 2)
        rotate(LAST, 0, 2)
        finish(LAST, 0, 2)
        second_product(LAST, 2, 4)
        rotate(LAST, 2, 4)
        finish(LAST, 2, 4)
